import numpy as np
import ml_dtypes


def mxq(x, axis, fmt="e4m3"):
    dtype, down = {"e4m3": (ml_dtypes.float8_e4m3fn, 7), "e5m2": (ml_dtypes.float8_e5m2, 14)}[fmt]
    v = np.moveaxis(np.asarray(x, np.float32).astype(ml_dtypes.bfloat16).astype(np.float64), axis, -1)
    blocks = v.reshape(v.shape[:-1] + (-1, 32))
    amax = np.abs(blocks).max(-1, keepdims=True)
    byte = np.maximum(np.where(amax > 0, np.frexp(amax)[1] - 1 + 127, 0) - down, 1)
    scale = np.exp2(byte - 127.0)
    codes = (blocks / scale).astype(np.float32).astype(dtype).astype(np.float64)
    return np.moveaxis((codes * scale).reshape(v.shape), -1, axis)


WIDE = False


def mx_kscale(k):
    if not WIDE:
        return np.ones(k)
    levels = np.array([10, -10, 5, -5, 0])
    if k % 512:
        return np.exp2(np.random.permutation(np.resize(levels, k // 32))).repeat(32)
    a = np.empty((k // 512, 16))
    for p in range(k // 512):
        a[p, :8] = np.random.permutation(np.resize(levels, 8))
        for g in range(8):
            far = levels[np.abs(levels - a[p, g]) >= 10]
            a[p, g + 8] = far[np.random.randint(len(far))]
    return np.exp2(a.ravel()).repeat(32)


BF16 = ml_dtypes.bfloat16


def bf(x):
    return np.asarray(x, np.float32).astype(BF16)


def f64(x):
    return np.asarray(x).astype(np.float64)


B, N, C, F = 4, 32, 1024, 1024
EPS_STD = 1e-5


def setup_inputs():
    u, s = mx_kscale(C), mx_kscale(C)
    rows = np.concatenate([u, u, s])
    return {"x": bf(np.random.standard_normal((B, N, C)) * u),
            "e_enc": bf(np.random.standard_normal((B, N, N, C)) * s),
            "W_pre": bf(np.random.standard_normal((3 * C, F)) / np.sqrt(3 * C) / rows[:, None]),
            "b_pre": bf(np.random.standard_normal(F) * 0.3)}


def core(x, e_enc, W_pre, b_pre):
    w = f64(W_pre)
    xq = mxq(f64(x), 2, "e4m3")
    tgt = xq @ mxq(w[:C], 0, "e4m3")
    src = xq @ mxq(w[C:2 * C], 0, "e4m3")
    edg = mxq(f64(e_enc), 3, "e4m3") @ mxq(w[2 * C:], 0, "e4m3")
    m = tgt[:, :, None, :] + src[:, None, :, :] + edg + f64(b_pre)
    mean = m.mean(axis=2)
    mn = m.min(axis=2)
    mx = m.max(axis=2)
    var = (m * m).mean(axis=2) - mean * mean
    std = np.sqrt(np.maximum(var, 0.0) + EPS_STD)
    return np.concatenate([mean, mn, mx, std], axis=-1)


def e4m3fn_bytes(y):
    return np.clip(np.asarray(y, np.float64), -448.0, 448.0).astype(np.float32).astype(ml_dtypes.float8_e4m3fn).view(np.uint8)


def reference(x, e_enc, W_pre, b_pre):
    out = core(x, e_enc, W_pre, b_pre)
    s = np.max(np.abs(out)) / 448.0
    return out, e4m3fn_bytes(out / s)

@@ -1,0 +1,410 @@
+from contextlib import ExitStack
+
+import concourse.mybir as mybir
+from concourse.masks import make_identity
+
+F32 = mybir.dt.float32
+BF16 = mybir.dt.bfloat16
+I32 = mybir.dt.int32
+U8 = mybir.dt.uint8
+FP8X4 = mybir.dt.float8_e4m3fn_x4
+FP8 = mybir.dt.float8_e4m3fn
+ALU = mybir.AluOpType
+ACT = mybir.ActivationFunctionType
+AX = mybir.AxisListType
+
+P = 128
+NJ = 32
+C = 1024
+F = 1024
+EPS_STD = 1e-5
+FLOPS = 2 * (4096 * 1024 * 1024 + 2 * 128 * 1024 * 1024)
+
+PHASES = ((0, 512, 256), (512, 256, 128), (768, 256, 128))
+JC = 8
+E_BUFS = 5
+VCOLS = 2816
+
+
+def tile_gnnlayer_pa_kernel(tc, x, e_enc, W_pre, b_pre, out_0, out_1):
+    nc = tc.nc
+    nph = len(PHASES)
+    x_rows = x.rearrange("b n c -> (b n) c")
+    e_rows = e_enc.rearrange("b i j c -> (b i) j c")
+    o0 = out_0.rearrange("b i (k f) -> (b i) k f", k=4)
+    o1 = out_1.rearrange("b i f -> (b i) f")
+
+    with ExitStack() as ctx:
+        ctx.enter_context(tc.manual_schedule())
+        const = ctx.enter_context(tc.tile_pool(name="const", bufs=1))
+        keep = ctx.enter_context(tc.tile_pool(name="keep", bufs=1))
+        sqp = ctx.enter_context(tc.tile_pool(name="sqp", bufs=3))
+        ps_tp = ctx.enter_context(tc.psum_pool(name="ps_tp", bufs=2))
+        ps_m = ctx.enter_context(tc.psum_pool(name="ps_m", bufs=4))
+        ps_ts = ctx.enter_context(tc.psum_pool(name="ps_ts", bufs=1))
+        ps_x = ctx.enter_context(tc.psum_pool(name="ps_x", bufs=1))
+
+        st = {}
+
+        ident = const.tile([P, P], F32, name="ident")
+        make_identity(nc, ident[:])
+        warm = const.tile([P, 2], F32, name="warm")
+        nc.vector.memset(warm[:], 1.0)
+        nc.scalar.activation(out=warm[:, 1:2], in_=warm[:, 0:1], func=ACT.Sqrt)
+        sel = const.tile([P, P], F32, name="sel")
+        nc.vector.memset(sel[:], 0.0)
+        for b in range(4):
+            nc.vector.memset(sel[32 * b : 32 * b + 32, 32 * b : 32 * b + 32], 1.0 / NJ)
+        pm = const.tile([P, 3 * nph], F32, name="pm")
+        b_bc = const.tile([P, F], BF16, name="b_bc")
+
+        def w_load(pool, u):
+            w, g, ph = u
+            c0, wd, nt = PHASES[ph]
+            raw = pool.tile([P, 4, wd], BF16, name="wraw", tag="wraw")
+            r0 = w * C + g * 512
+            nc.sync.dma_start(out=raw[:], in_=W_pre[r0 : r0 + 512, c0 : c0 + wd].rearrange("(p t) f -> p t f", t=4))
+            st[("wraw", u)] = raw
+
+        def w_interleave(pool, u, eng):
+            wd = PHASES[u[2]][1]
+            raw = st[("wraw", u)]
+            grp = pool.tile([P, wd, 4], BF16, name="wgrp", tag="wgrp", align_bytes=64)
+            src = raw[:].rearrange("p t f -> p f t")
+            if eng == "v":
+                nc.vector.tensor_copy(out=grp[:], in_=src)
+            elif eng == "s":
+                nc.scalar.copy(out=grp[:], in_=src)
+            else:
+                nc.gpsimd.tensor_scalar(out=grp[:], in0=src, scalar1=1.0, scalar2=0.0, op0=ALU.mult, op1=ALU.add)
+            st[("wgrp", u)] = grp
+
+        def w_quant(u):
+            wd = PHASES[u[2]][1]
+            grp = st[("wgrp", u)]
+            wc = keep.tile([P, wd], I32, name="wc%d%d%d" % u, align_bytes=64)
+            ws = keep.tile([P, wd], U8, name="ws%d%d%d" % u, align_bytes=64)
+            nc.vector.quantize_mx(out=wc[:].bitcast(FP8X4), scales=ws[:], in_=grp[:].rearrange("p f t -> p (f t)"))
+            st[("wc", u)] = wc
+            st[("ws", u)] = ws
+
+        def e_load(pool, s):
+            er = pool.tile([P, 2, C], BF16, name="er", tag="er")
+            nc.sync.dma_start(out=er[:], in_=e_rows[:, 2 * s : 2 * s + 2, :])
+            st[("er", s)] = er
+
+        def transpose4(words, base):
+            tp = ps_tp.tile([P, 2, 2, P], F32, name="tp", tag="tp")
+            for g in range(2):
+                for u in range(2):
+                    lo = base + 256 * g
+                    nc.tensor.transpose(tp[:, g, u, :], words[:, lo + u : lo + 256 : 2], ident[:])
+            return tp
+
+        def e_transpose(s):
+            words = st[("er", s)][:].rearrange("p j c -> p (j c)").bitcast(F32)
+            for jj in range(2):
+                st[("tp", s, jj)] = transpose4(words, 512 * jj)
+
+        def e_copy(pool, s):
+            eg = pool.tile([P, 2, 2, P, 4], BF16, name="eg", tag="eg", align_bytes=64)
+            for jj in range(2):
+                nc.scalar.copy(out=eg[:, jj].bitcast(F32), in_=st[("tp", s, jj)][:].rearrange("p g u r -> p g r u"))
+            st[("eg", s)] = eg
+
+        def e_quant(s):
+            ec = keep.tile([P, 4 * P], I32, name="ec%d" % s, align_bytes=64)
+            es = keep.tile([P, 4 * P], U8, name="es%d" % s, align_bytes=64)
+            nc.vector.quantize_mx(
+                out=ec[:].bitcast(FP8X4), scales=es[:], in_=st[("eg", s)][:].rearrange("p j g r t -> p (j g r t)")
+            )
+            st[("ec", s)] = ec
+            st[("es", s)] = es
+
+        x_sb = const.tile([P, C], BF16, name="x_sb")
+        xg = const.tile([P, 2, P, 4], BF16, name="xg", align_bytes=64)
+        xc = const.tile([P, 2 * P], I32, name="xc", align_bytes=64)
+        xs = const.tile([P, 2 * P], U8, name="xs", align_bytes=64)
+        xs4 = const.tile([P, 2 * P, 4], U8, name="xs4", align_bytes=64)
+
+        def x_repeat(c):
+            xr = keep.tile([P, JC, 2, P], I32, name="xr%d" % c, align_bytes=64)
+            xrs = keep.tile([P, JC, 2, P], U8, name="xrs%d" % c, align_bytes=64)
+            codes = xc[:].rearrange("p (g b n) -> p g n b", g=2, b=4)
+            words = xs4[:].rearrange("p c r -> p (c r)").bitcast(I32).rearrange("p (g b n) -> p g n b", g=2, b=4)
+            for g in range(2):
+                nc.vector.tensor_copy(
+                    out=xr[:, :, g, :].rearrange("p j (b i) -> p j b i", b=4),
+                    in_=codes[:, g, c * JC : (c + 1) * JC, :].unsqueeze(3).to_broadcast([P, JC, 4, 32]),
+                )
+                nc.vector.tensor_copy(
+                    out=xrs[:, :, g, :].bitcast(I32).rearrange("p j (b r) -> p j b r", b=4),
+                    in_=words[:, g, c * JC : (c + 1) * JC, :].unsqueeze(3).to_broadcast([P, JC, 4, 8]),
+                )
+            st[("xr", c)] = xr
+            st[("xrs", c)] = xrs
+
+        def mx(out, lhsT, lhsT_scale, u, n, start, stop):
+            nc.tensor.matmul_mx(
+                out=out,
+                lhsT=lhsT.bitcast(FP8X4),
+                lhsT_scale=lhsT_scale,
+                rhs=st[("wc", u)][:, 0:n].bitcast(FP8X4),
+                rhs_scale=st[("ws", u)][:, 0:n],
+                start=start,
+                stop=stop,
+            )
+
+        def matmuls(ph, j):
+            c0, wd, nt = PHASES[ph]
+            s, jj = divmod(j, 2)
+            c, jc = divmod(j, JC)
+            mb = ps_m.tile([P, wd], F32, name="mb", tag="mb")
+            st[("mb", ph, j)] = mb
+            for g in range(2):
+                cols = slice((2 * jj + g) * P, (2 * jj + g + 1) * P)
+                mx(mb[:], st[("ec", s)][:, cols], st[("es", s)][:, cols], (2, g, ph), wd, g == 0, False)
+            for g in range(2):
+                mx(mb[:], st[("xr", c)][:, jc, g, :], st[("xrs", c)][:, jc, g, :], (1, g, ph), wd, False, g == 1)
+            if nt:
+                for g in range(2):
+                    cols = slice((2 * jj + g) * P, (2 * jj + g + 1) * P)
+                    mx(
+                        st[("ts", ph)][:], st[("ec", s)][:, cols], st[("es", s)][:, cols], (2, g, ph), nt,
+                        j == 0 and g == 0, j == NJ - 1 and g == 1,
+                    )
+
+        def e_vec(ph, j):
+            c0, wd, nt = PHASES[ph]
+            mb = st[("mb", ph, j)]
+            rmax, rmin, vs = st[("rmax", ph)], st[("rmin", ph)], st[("vs", ph)]
+            if j == 0:
+                nc.vector.tensor_copy(out=rmax[:], in_=mb[:])
+                nc.vector.tensor_copy(out=rmin[:], in_=mb[:])
+                if nt < wd:
+                    nc.vector.tensor_copy(out=vs[:, nt:wd], in_=mb[:, nt:wd])
+            else:
+                nc.vector.tensor_tensor(out=rmax[:], in0=mb[:], in1=rmax[:], op=ALU.max)
+                nc.vector.tensor_tensor(out=rmin[:], in0=mb[:], in1=rmin[:], op=ALU.min)
+                if nt < wd:
+                    nc.vector.tensor_tensor(out=vs[:, nt:wd], in0=mb[:, nt:wd], in1=vs[:, nt:wd], op=ALU.add)
+
+        def e_sq(ph, j):
+            wd = PHASES[ph][1]
+            s, jj = divmod(j, 2)
+            if s == 0:
+                dst = st[("acc", ph)]
+            else:
+                if jj == 0:
+                    st[("sq", ph, s)] = sqp.tile([P, 2, wd], F32, name="sq", tag="sq")
+                dst = st[("sq", ph, s)]
+            nc.scalar.activation(out=dst[:, jj, :], in_=st[("mb", ph, j)][:], func=ACT.Square)
+
+        def e_acc(ph, s):
+            if s > 0:
+                acc = st[("acc", ph)]
+                nc.gpsimd.tensor_tensor(out=acc[:], in0=acc[:], in1=st[("sq", ph, s)][:], op=ALU.add)
+
+        def phase_tiles(ph):
+            c0, wd, nt = PHASES[ph]
+            for nm in ("rmax", "rmin", "vs", "tb"):
+                st[(nm, ph)] = keep.tile([P, wd], F32, name="%s%d" % (nm, ph))
+            st[("acc", ph)] = keep.tile([P, 2, wd], F32, name="acc%d" % ph)
+            if nt:
+                st[("srcm", ph)] = keep.tile([P, nt], F32, name="srcm%d" % ph)
+                st[("srcs", ph)] = keep.tile([P, nt], F32, name="srcs%d" % ph)
+                if ph % 2 == 0:
+                    st[("ts", ph)] = ps_ts.tile([P, nt], F32, name="ts", tag="ts")
+                else:
+                    st[("ts", ph)] = ps_tp.tile([P, nt], F32, name="tp", tag="tp")
+
+        def x_product(w, ph, n):
+            acc = ps_x.tile([P, n], F32, name="px", tag="px")
+            for g in range(2):
+                mx(acc[:], xc[:, g * P : (g + 1) * P], xs[:, g * P : (g + 1) * P], (w, g, ph), n, g == 0, g == 1)
+            return acc
+
+        def src_a(ph):
+            nt = PHASES[ph][2]
+            if nt:
+                nc.scalar.copy(out=st[("srcs", ph)][:], in_=x_product(1, ph, nt)[:])
+
+        def src_b(ph):
+            nt = PHASES[ph][2]
+            if nt:
+                sm = ps_x.tile([P, nt], F32, name="px", tag="px")
+                nc.tensor.matmul(out=sm[:], lhsT=sel[:], rhs=st[("srcs", ph)][:], start=True, stop=True)
+                nc.scalar.copy(out=st[("srcm", ph)][:], in_=sm[:])
+
+        def tgt(ph):
+            c0, wd, nt = PHASES[ph]
+            nc.vector.tensor_tensor(out=st[("tb", ph)][:], in0=x_product(0, ph, wd)[:], in1=b_bc[:, c0 : c0 + wd], op=ALU.add)
+
+        def fin_a(fin, O, ph):
+            c0, wd, nt = PHASES[ph]
+            cols = slice(c0, c0 + wd)
+            tb = st[("tb", ph)]
+            nc.vector.tensor_tensor(out=O[:, 2, cols], in0=st[("rmax", ph)][:], in1=tb[:], op=ALU.add)
+            nc.gpsimd.tensor_tensor(out=O[:, 1, cols], in0=st[("rmin", ph)][:], in1=tb[:], op=ALU.add)
+            a = fin.tile([P, wd], F32, name="a", tag="a")
+            a2 = fin.tile([P, wd], F32, name="a2", tag="a2")
+            q = fin.tile([P, wd], F32, name="q", tag="q")
+            if nt:
+                nc.vector.scalar_tensor_tensor(
+                    out=a[:, 0:nt], in0=st[("ts", ph)][:], scalar=1.0 / NJ, in1=st[("srcm", ph)][:], op0=ALU.mult, op1=ALU.add
+                )
+            if nt < wd:
+                nc.scalar.mul(out=a[:, nt:wd], in_=st[("vs", ph)][:, nt:wd], mul=1.0 / NJ)
+            nc.scalar.activation(out=a2[:], in_=a[:], func=ACT.Square)
+            acc = st[("acc", ph)]
+            nc.gpsimd.tensor_tensor(out=q[:], in0=acc[:, 0, :], in1=acc[:, 1, :], op=ALU.add)
+            nc.gpsimd.tensor_tensor(out=O[:, 0, cols], in0=a[:], in1=tb[:], op=ALU.add)
+            st[("a2", ph)] = a2
+            st[("q", ph)] = q
+
+        def fin_b(fin, O, ph):
+            c0, wd, nt = PHASES[ph]
+            var = fin.tile([P, wd], F32, name="var", tag="var")
+            nc.vector.scalar_tensor_tensor(
+                out=var[:], in0=st[("q", ph)][:], scalar=1.0 / NJ, in1=st[("a2", ph)][:], op0=ALU.mult, op1=ALU.subtract
+            )
+            nc.vector.tensor_scalar(out=var[:], in0=var[:], scalar1=0.0, scalar2=EPS_STD, op0=ALU.max, op1=ALU.add)
+            nc.scalar.activation(out=O[:, 3, c0 : c0 + wd], in_=var[:], func=ACT.Sqrt)
+
+        def fin_c(fin, O, ph):
+            c0, wd, nt = PHASES[ph]
+            cols = slice(c0, c0 + wd)
+            for n, k in enumerate((2, 1, 3)):
+                nc.vector.tensor_reduce(
+                    out=pm[:, 3 * ph + n : 3 * ph + n + 1], in_=O[:, k, cols], axis=AX.X, op=ALU.max, apply_absolute_value=True
+                )
+            nc.sync.dma_start(out=o0[:, :, cols], in_=O[:, :, cols])
+
+        def run_phase(ph, prep, hooks):
+            for s in range(NJ // 2):
+                prep(s)
+                for h in hooks.get(s, ()):
+                    h()
+                for jj in range(2):
+                    j = 2 * s + jj
+                    matmuls(ph, j)
+                    e_vec(ph, j)
+                    e_sq(ph, j)
+                e_acc(ph, s)
+
+        def own_hooks(ph):
+            return {1: [lambda: src_a(ph)], 3: [lambda: src_b(ph)], 5: [lambda: tgt(ph)]}
+
+        lazy = [(0, 0, 0), (0, 1, 0)]
+        for ph in range(1, nph):
+            lazy.extend([(2, 0, ph), (2, 1, ph), (1, 0, ph), (1, 1, ph), (0, 0, ph), (0, 1, ph)])
+
+        with ExitStack() as c1:
+            erp = c1.enter_context(tc.tile_pool(name="erp", bufs=E_BUFS))
+            egp = c1.enter_context(tc.tile_pool(name="egp", bufs=3))
+            wrp = c1.enter_context(tc.tile_pool(name="wrp", bufs=4))
+            wgp = c1.enter_context(tc.tile_pool(name="wgp", bufs=3))
+
+            nc.sync.dma_start(out=x_sb[:], in_=x_rows)
+            w_load(wrp, (2, 0, 0))
+            w_load(wrp, (2, 1, 0))
+            e_load(erp, 0)
+            w_load(wrp, (1, 0, 0))
+            w_load(wrp, (1, 1, 0))
+            e_load(erp, 1)
+            e_load(erp, 2)
+            nc.sync.dma_start(out=b_bc[:], in_=b_pre.partition_broadcast(P))
+            for s in range(3, E_BUFS):
+                e_load(erp, s)
+
+            tpx = transpose4(x_sb[:].bitcast(F32), 0)
+            nc.scalar.copy(out=xg[:].bitcast(F32), in_=tpx[:].rearrange("p g u r -> p g r u"))
+            nc.vector.memset(xs[:].bitcast(I32), 0)
+            w_interleave(wgp, (2, 0, 0), "v")
+            w_interleave(wgp, (2, 1, 0), "g")
+            nc.vector.quantize_mx(out=xc[:].bitcast(FP8X4), scales=xs[:], in_=xg[:].rearrange("p g r t -> p (g r t)"))
+            w_quant((2, 0, 0))
+            e_transpose(0)
+            e_copy(egp, 0)
+            e_load(erp, E_BUFS)
+            for r in range(4):
+                nc.vector.tensor_copy(out=xs4[:, :, r], in_=xs[:])
+            x_repeat(0)
+            w_quant((2, 1, 0))
+            w_interleave(wgp, (1, 0, 0), "v")
+            w_interleave(wgp, (1, 1, 0), "s")
+            e_quant(0)
+            w_quant((1, 0, 0))
+            e_transpose(1)
+            e_copy(egp, 1)
+            e_load(erp, E_BUFS + 1)
+            w_quant((1, 1, 0))
+            w_load(wrp, lazy[0])
+            phase_tiles(0)
+
+            def prep0(s):
+                if s + 2 < NJ // 2:
+                    e_transpose(s + 2)
+                    e_copy(egp, s + 2)
+                    if s + 2 + E_BUFS < NJ // 2:
+                        e_load(erp, s + 2 + E_BUFS)
+                if s + 1 < NJ // 2:
+                    e_quant(s + 1)
+                if s + 1 < len(lazy):
+                    w_load(wrp, lazy[s + 1])
+                if s < len(lazy):
+                    w_interleave(wgp, lazy[s], "s")
+                if 1 <= s <= len(lazy):
+                    w_quant(lazy[s - 1])
+                if s % 4 == 1 and s // 4 + 1 < NJ // JC:
+                    x_repeat(s // 4 + 1)
+
+            run_phase(0, prep0, own_hooks(0))
+
+        with ExitStack() as c2:
+            fin = c2.enter_context(tc.tile_pool(name="fin", bufs=2))
+            one = c2.enter_context(tc.tile_pool(name="one", bufs=1))
+            O = one.tile([P, 4, F], F32, name="O")
+            o8 = one.tile([P, 4 * F], FP8, name="o8")
+
+            def before(ph):
+                return {
+                    0: [lambda: fin_a(fin, O, ph)],
+                    4: [lambda: fin_b(fin, O, ph)],
+                    6: [lambda: fin_c(fin, O, ph)],
+                }
+
+            for ph in range(1, nph):
+                phase_tiles(ph)
+                hooks = own_hooks(ph)
+                prev = before(ph - 1)
+                for s in (0, 4, 6):
+                    hooks[s] = hooks.get(s, []) + prev[s]
+                run_phase(ph, lambda s: None, hooks)
+            fin_a(fin, O, nph - 1)
+            fin_b(fin, O, nph - 1)
+            fin_c(fin, O, nph - 1)
+
+            sc1 = one.tile([P, 4], F32, name="sc1")
+            nc.vector.tensor_reduce(out=sc1[:, 0:1], in_=pm[:], axis=AX.X, op=ALU.max)
+            am = ps_x.tile([P, P], F32, name="px", tag="px")
+            nc.tensor.transpose(am[:], sc1[:, 0:1].to_broadcast([P, P]), ident[:])
+            nc.vector.tensor_reduce(out=sc1[:, 1:2], in_=am[:], axis=AX.X, op=ALU.max)
+            nc.vector.reciprocal(out=sc1[:, 2:3], in_=sc1[:, 1:2])
+            nc.vector.tensor_scalar(out=sc1[:, 3:4], in0=sc1[:, 2:3], scalar1=448.0, scalar2=None, op0=ALU.mult)
+            fac = sc1[:, 3:4]
+
+            flat = O[:].rearrange("p k f -> p (k f)")
+            vh = VCOLS // 2
+            sh = (4 * F - VCOLS) // 2
+            for h in range(2):
+                va = h * vh
+                sa = VCOLS + h * sh
+                tv = fin.tile([P, vh], F32, name="tv", tag="tv")
+                tsc = fin.tile([P, sh], F32, name="tsc", tag="tsc")
+                nc.vector.tensor_scalar(out=tv[:], in0=flat[:, va : va + vh], scalar1=fac, scalar2=None, op0=ALU.mult)
+                nc.scalar.activation(out=tsc[:], in_=flat[:, sa : sa + sh], func=ACT.Copy, scale=fac)
+                nc.vector.tensor_copy(out=o8[:, va : va + vh], in_=tv[:], saturate=False)
+                nc.scalar.copy(out=o8[:, sa : sa + sh], in_=tsc[:], saturate=False)
+                nc.sync.dma_start(out=o1[:, va : va + vh], in_=o8[:, va : va + vh].bitcast(U8))
+                nc.sync.dma_start(out=o1[:, sa : sa + sh], in_=o8[:, sa : sa + sh].bitcast(U8))

@@ -21,8 +21,10 @@ EPS_STD = 1e-5
 FLOPS = 2 * (4096 * 1024 * 1024 + 2 * 128 * 1024 * 1024)
 
 PHASES = ((0, 512, 256), (512, 256, 128), (768, 256, 128))
-JC = 8
+JC = 4
+SQ_SCALE = (1.0 / 32.0) ** 0.5
 E_BUFS = 5
+LAZY_COLS = 256
 VCOLS = 2816
 
 
@@ -55,6 +57,8 @@ def tile_gnnlayer_pa_kernel(tc, x, e_enc, W_pre, b_pre, out_0, out_1):
         nc.vector.memset(sel[:], 0.0)
         for b in range(4):
             nc.vector.memset(sel[32 * b : 32 * b + 32, 32 * b : 32 * b + 32], 1.0 / NJ)
+        eps = const.tile([P, 1], F32, name="eps")
+        nc.vector.memset(eps[:], EPS_STD)
         pm = const.tile([P, 3 * nph], F32, name="pm")
         b_bc = const.tile([P, F], BF16, name="b_bc")
 
@@ -155,17 +159,21 @@ def tile_gnnlayer_pa_kernel(tc, x, e_enc, W_pre, b_pre, out_0, out_1):
                 stop=stop,
             )
 
-        def matmuls(ph, j):
+        def mm_x(ph, j):
+            wd = PHASES[ph][1]
+            c, jc = divmod(j, JC)
+            mb = st[("mb", ph, j)]
+            for g in range(2):
+                mx(mb[:], st[("xr", c)][:, jc, g, :], st[("xrs", c)][:, jc, g, :], (1, g, ph), wd, False, g == 1)
+
+        def mm_e(ph, j):
             c0, wd, nt = PHASES[ph]
             s, jj = divmod(j, 2)
-            c, jc = divmod(j, JC)
             mb = ps_m.tile([P, wd], F32, name="mb", tag="mb")
             st[("mb", ph, j)] = mb
             for g in range(2):
                 cols = slice((2 * jj + g) * P, (2 * jj + g + 1) * P)
                 mx(mb[:], st[("ec", s)][:, cols], st[("es", s)][:, cols], (2, g, ph), wd, g == 0, False)
-            for g in range(2):
-                mx(mb[:], st[("xr", c)][:, jc, g, :], st[("xrs", c)][:, jc, g, :], (1, g, ph), wd, False, g == 1)
             if nt:
                 for g in range(2):
                     cols = slice((2 * jj + g) * P, (2 * jj + g + 1) * P)
@@ -179,15 +187,13 @@ def tile_gnnlayer_pa_kernel(tc, x, e_enc, W_pre, b_pre, out_0, out_1):
             mb = st[("mb", ph, j)]
             rmax, rmin, vs = st[("rmax", ph)], st[("rmin", ph)], st[("vs", ph)]
             if j == 0:
-                nc.vector.tensor_copy(out=rmax[:], in_=mb[:])
-                nc.vector.tensor_copy(out=rmin[:], in_=mb[:])
-                if nt < wd:
-                    nc.vector.tensor_copy(out=vs[:, nt:wd], in_=mb[:, nt:wd])
+                nc.scalar.copy(out=st[("m0", ph)][:], in_=mb[:])
             else:
-                nc.vector.tensor_tensor(out=rmax[:], in0=mb[:], in1=rmax[:], op=ALU.max)
-                nc.vector.tensor_tensor(out=rmin[:], in0=mb[:], in1=rmin[:], op=ALU.min)
+                m0 = st[("m0", ph)]
+                nc.vector.tensor_tensor(out=rmax[:], in0=mb[:], in1=(m0 if j == 1 else rmax)[:], op=ALU.max)
+                nc.vector.tensor_tensor(out=rmin[:], in0=mb[:], in1=(m0 if j == 1 else rmin)[:], op=ALU.min)
                 if nt < wd:
-                    nc.vector.tensor_tensor(out=vs[:, nt:wd], in0=mb[:, nt:wd], in1=vs[:, nt:wd], op=ALU.add)
+                    nc.vector.tensor_tensor(out=vs[:, nt:wd], in0=mb[:, nt:wd], in1=(m0 if j == 1 else vs)[:, nt:wd], op=ALU.add)
 
         def e_sq(ph, j):
             wd = PHASES[ph][1]
@@ -198,17 +204,18 @@ def tile_gnnlayer_pa_kernel(tc, x, e_enc, W_pre, b_pre, out_0, out_1):
                 if jj == 0:
                     st[("sq", ph, s)] = sqp.tile([P, 2, wd], F32, name="sq", tag="sq")
                 dst = st[("sq", ph, s)]
-            nc.scalar.activation(out=dst[:, jj, :], in_=st[("mb", ph, j)][:], func=ACT.Square)
+            nc.scalar.activation(out=dst[:, jj, :], in_=st[("mb", ph, j)][:], func=ACT.Square, scale=SQ_SCALE)
 
         def e_acc(ph, s):
-            if s > 0:
+            if 0 < s < NJ // 2 - 1:
                 acc = st[("acc", ph)]
                 nc.gpsimd.tensor_tensor(out=acc[:], in0=acc[:], in1=st[("sq", ph, s)][:], op=ALU.add)
 
         def phase_tiles(ph):
             c0, wd, nt = PHASES[ph]
-            for nm in ("rmax", "rmin", "vs", "tb"):
+            for nm in ("rmax", "rmin", "vs", "tb", "q"):
                 st[(nm, ph)] = keep.tile([P, wd], F32, name="%s%d" % (nm, ph))
+            st[("m0", ph)] = st[("q", ph)]
             st[("acc", ph)] = keep.tile([P, 2, wd], F32, name="acc%d" % ph)
             if nt:
                 st[("srcm", ph)] = keep.tile([P, nt], F32, name="srcm%d" % ph)
@@ -240,15 +247,10 @@ def tile_gnnlayer_pa_kernel(tc, x, e_enc, W_pre, b_pre, out_0, out_1):
             c0, wd, nt = PHASES[ph]
             nc.vector.tensor_tensor(out=st[("tb", ph)][:], in0=x_product(0, ph, wd)[:], in1=b_bc[:, c0 : c0 + wd], op=ALU.add)
 
-        def fin_a(fin, O, ph):
+        def fin_mean(fin, ph):
             c0, wd, nt = PHASES[ph]
-            cols = slice(c0, c0 + wd)
-            tb = st[("tb", ph)]
-            nc.vector.tensor_tensor(out=O[:, 2, cols], in0=st[("rmax", ph)][:], in1=tb[:], op=ALU.add)
-            nc.gpsimd.tensor_tensor(out=O[:, 1, cols], in0=st[("rmin", ph)][:], in1=tb[:], op=ALU.add)
             a = fin.tile([P, wd], F32, name="a", tag="a")
             a2 = fin.tile([P, wd], F32, name="a2", tag="a2")
-            q = fin.tile([P, wd], F32, name="q", tag="q")
             if nt:
                 nc.vector.scalar_tensor_tensor(
                     out=a[:, 0:nt], in0=st[("ts", ph)][:], scalar=1.0 / NJ, in1=st[("srcm", ph)][:], op0=ALU.mult, op1=ALU.add
@@ -256,48 +258,80 @@ def tile_gnnlayer_pa_kernel(tc, x, e_enc, W_pre, b_pre, out_0, out_1):
             if nt < wd:
                 nc.scalar.mul(out=a[:, nt:wd], in_=st[("vs", ph)][:, nt:wd], mul=1.0 / NJ)
             nc.scalar.activation(out=a2[:], in_=a[:], func=ACT.Square)
-            acc = st[("acc", ph)]
-            nc.gpsimd.tensor_tensor(out=q[:], in0=acc[:, 0, :], in1=acc[:, 1, :], op=ALU.add)
-            nc.gpsimd.tensor_tensor(out=O[:, 0, cols], in0=a[:], in1=tb[:], op=ALU.add)
+            st[("a", ph)] = a
             st[("a2", ph)] = a2
-            st[("q", ph)] = q
 
-        def fin_b(fin, O, ph):
-            c0, wd, nt = PHASES[ph]
-            var = fin.tile([P, wd], F32, name="var", tag="var")
-            nc.vector.scalar_tensor_tensor(
-                out=var[:], in0=st[("q", ph)][:], scalar=1.0 / NJ, in1=st[("a2", ph)][:], op0=ALU.mult, op1=ALU.subtract
-            )
-            nc.vector.tensor_scalar(out=var[:], in0=var[:], scalar1=0.0, scalar2=EPS_STD, op0=ALU.max, op1=ALU.add)
-            nc.scalar.activation(out=O[:, 3, c0 : c0 + wd], in_=var[:], func=ACT.Sqrt)
+        def fin_q(ph):
+            acc = st[("acc", ph)]
+            nc.gpsimd.tensor_tensor(out=st[("q", ph)][:], in0=acc[:, 0, :], in1=acc[:, 1, :], op=ALU.add)
 
-        def fin_c(fin, O, ph):
+        def fin_minmax(O, ph):
             c0, wd, nt = PHASES[ph]
             cols = slice(c0, c0 + wd)
-            for n, k in enumerate((2, 1, 3)):
-                nc.vector.tensor_reduce(
-                    out=pm[:, 3 * ph + n : 3 * ph + n + 1], in_=O[:, k, cols], axis=AX.X, op=ALU.max, apply_absolute_value=True
-                )
-            nc.sync.dma_start(out=o0[:, :, cols], in_=O[:, :, cols])
+            tb = st[("tb", ph)]
+            nc.vector.tensor_tensor(out=O[:, 2, cols], in0=st[("rmax", ph)][:], in1=tb[:], op=ALU.add)
+            nc.vector.tensor_tensor(out=O[:, 1, cols], in0=st[("rmin", ph)][:], in1=tb[:], op=ALU.add)
 
-        def run_phase(ph, prep, hooks):
+        def fin_std(fin, O, ph):
+            c0, wd, nt = PHASES[ph]
+            var = fin.tile([P, wd], F32, name="var", tag="var")
+            q = st[("q", ph)]
+            sq = st[("sq", ph, NJ // 2 - 1)]
+            nc.vector.tensor_tensor(out=q[:], in0=q[:], in1=sq[:, 0, :], op=ALU.add)
+            nc.vector.tensor_tensor(out=q[:], in0=q[:], in1=sq[:, 1, :], op=ALU.add)
+            nc.vector.tensor_tensor(out=var[:], in0=q[:], in1=st[("a2", ph)][:], op=ALU.subtract)
+            nc.scalar.activation(out=var[:], in_=var[:], func=ACT.Relu)
+            nc.scalar.activation(out=O[:, 3, c0 : c0 + wd], in_=var[:], func=ACT.Sqrt, bias=eps[:, 0:1])
+
+        def fin_meanout(O, ph):
+            c0, wd, nt = PHASES[ph]
+            nc.vector.tensor_tensor(out=O[:, 0, c0 : c0 + wd], in0=st[("a", ph)][:], in1=st[("tb", ph)][:], op=ALU.add)
+
+        def fin_amax(O, ph, n, k):
+            c0, wd, nt = PHASES[ph]
+            nc.vector.tensor_reduce(
+                out=pm[:, 3 * ph + n : 3 * ph + n + 1], in_=O[:, k, c0 : c0 + wd], axis=AX.X, op=ALU.max, apply_absolute_value=True
+            )
+
+        def fin_store(O, ph):
+            c0, wd, nt = PHASES[ph]
+            nc.sync.dma_start(out=o0[:, :, c0 : c0 + wd], in_=O[:, :, c0 : c0 + wd])
+
+        def wd_of(ph):
+            return PHASES[ph][1]
+
+        def run_phase(ph, prep, step_hooks, bank_hooks):
             for s in range(NJ // 2):
                 prep(s)
-                for h in hooks.get(s, ()):
+                for h in step_hooks.get(s, ()):
                     h()
                 for jj in range(2):
                     j = 2 * s + jj
-                    matmuls(ph, j)
+                    if not (ph == 0 and s == 0):
+                        mm_e(ph, j)
+                    mm_x(ph, j)
                     e_vec(ph, j)
                     e_sq(ph, j)
+                    for h in bank_hooks.get(j, ()):
+                        h()
                 e_acc(ph, s)
 
         def own_hooks(ph):
-            return {1: [lambda: src_a(ph)], 3: [lambda: src_b(ph)], 5: [lambda: tgt(ph)]}
+            return {1: [lambda: src_a(ph)], 3: [lambda: src_b(ph)], 5: [lambda: tgt(ph)], NJ // 2 - 1: [lambda: fin_q(ph)]}
 
         lazy = [(0, 0, 0), (0, 1, 0)]
         for ph in range(1, nph):
             lazy.extend([(2, 0, ph), (2, 1, ph), (1, 0, ph), (1, 1, ph), (0, 0, ph), (0, 1, ph)])
+
+        lazy_at = {}
+        step, room = 0, LAZY_COLS
+        for u in lazy:
+            wd = PHASES[u[2]][1]
+            if wd > room and room < LAZY_COLS:
+                step, room = step + 1, LAZY_COLS
+            lazy_at.setdefault(step, []).append(u)
+            room -= wd
+        assert step <= NJ // 2 - 2
 
         with ExitStack() as c1:
             erp = c1.enter_context(tc.tile_pool(name="erp", bufs=E_BUFS))
@@ -305,10 +339,10 @@ def tile_gnnlayer_pa_kernel(tc, x, e_enc, W_pre, b_pre, out_0, out_1):
             wrp = c1.enter_context(tc.tile_pool(name="wrp", bufs=4))
             wgp = c1.enter_context(tc.tile_pool(name="wgp", bufs=3))
 
-            nc.sync.dma_start(out=x_sb[:], in_=x_rows)
             w_load(wrp, (2, 0, 0))
-            w_load(wrp, (2, 1, 0))
+            nc.sync.dma_start(out=x_sb[:], in_=x_rows)
             e_load(erp, 0)
+            w_load(wrp, (2, 1, 0))
             w_load(wrp, (1, 0, 0))
             w_load(wrp, (1, 1, 0))
             e_load(erp, 1)
@@ -317,30 +351,33 @@ def tile_gnnlayer_pa_kernel(tc, x, e_enc, W_pre, b_pre, out_0, out_1):
             for s in range(3, E_BUFS):
                 e_load(erp, s)
 
-            tpx = transpose4(x_sb[:].bitcast(F32), 0)
-            nc.scalar.copy(out=xg[:].bitcast(F32), in_=tpx[:].rearrange("p g u r -> p g r u"))
             nc.vector.memset(xs[:].bitcast(I32), 0)
             w_interleave(wgp, (2, 0, 0), "v")
-            w_interleave(wgp, (2, 1, 0), "g")
-            nc.vector.quantize_mx(out=xc[:].bitcast(FP8X4), scales=xs[:], in_=xg[:].rearrange("p g r t -> p (g r t)"))
-            w_quant((2, 0, 0))
+            tpx = transpose4(x_sb[:].bitcast(F32), 0)
+            nc.scalar.copy(out=xg[:].bitcast(F32), in_=tpx[:].rearrange("p g u r -> p g r u"))
             e_transpose(0)
             e_copy(egp, 0)
             e_load(erp, E_BUFS)
+            w_interleave(wgp, (2, 1, 0), "s")
+            nc.vector.quantize_mx(out=xc[:].bitcast(FP8X4), scales=xs[:], in_=xg[:].rearrange("p g r t -> p (g r t)"))
+            w_quant((2, 0, 0))
             for r in range(4):
                 nc.vector.tensor_copy(out=xs4[:, :, r], in_=xs[:])
+            e_quant(0)
             x_repeat(0)
             w_quant((2, 1, 0))
             w_interleave(wgp, (1, 0, 0), "v")
             w_interleave(wgp, (1, 1, 0), "s")
-            e_quant(0)
-            w_quant((1, 0, 0))
             e_transpose(1)
             e_copy(egp, 1)
             e_load(erp, E_BUFS + 1)
+            w_quant((1, 0, 0))
             w_quant((1, 1, 0))
-            w_load(wrp, lazy[0])
+            for u in lazy_at[0]:
+                w_load(wrp, u)
             phase_tiles(0)
+            mm_e(0, 0)
+            mm_e(0, 1)
 
             def prep0(s):
                 if s + 2 < NJ // 2:
@@ -348,18 +385,19 @@ def tile_gnnlayer_pa_kernel(tc, x, e_enc, W_pre, b_pre, out_0, out_1):
                     e_copy(egp, s + 2)
                     if s + 2 + E_BUFS < NJ // 2:
                         e_load(erp, s + 2 + E_BUFS)
+                for u in lazy_at.get(s + 1, ()):
+                    w_load(wrp, u)
+                for u in lazy_at.get(s, ()):
+                    w_interleave(wgp, u, "s")
+                for u in lazy_at.get(s - 1, ()):
+                    w_quant(u)
                 if s + 1 < NJ // 2:
                     e_quant(s + 1)
-                if s + 1 < len(lazy):
-                    w_load(wrp, lazy[s + 1])
-                if s < len(lazy):
-                    w_interleave(wgp, lazy[s], "s")
-                if 1 <= s <= len(lazy):
-                    w_quant(lazy[s - 1])
-                if s % 4 == 1 and s // 4 + 1 < NJ // JC:
-                    x_repeat(s // 4 + 1)
+                if s == 0:
+                    for c in range(1, NJ // JC):
+                        x_repeat(c)
 
-            run_phase(0, prep0, own_hooks(0))
+            run_phase(0, prep0, own_hooks(0), {})
 
         with ExitStack() as c2:
             fin = c2.enter_context(tc.tile_pool(name="fin", bufs=2))
@@ -367,23 +405,38 @@ def tile_gnnlayer_pa_kernel(tc, x, e_enc, W_pre, b_pre, out_0, out_1):
             O = one.tile([P, 4, F], F32, name="O")
             o8 = one.tile([P, 4 * F], FP8, name="o8")
 
-            def before(ph):
-                return {
-                    0: [lambda: fin_a(fin, O, ph)],
-                    4: [lambda: fin_b(fin, O, ph)],
-                    6: [lambda: fin_c(fin, O, ph)],
-                }
+            def at_start(ph):
+                fin_mean(fin, ph)
+
+            def in_window(ph):
+                fin_minmax(O, ph)
+                fin_meanout(O, ph)
+                fin_std(fin, O, ph)
+
+            def later(ph):
+                for n, k in enumerate((2, 1, 3)):
+                    fin_amax(O, ph, n, k)
+                fin_store(O, ph)
+
+            def hooks_for(ph):
+                steps = own_hooks(ph)
+                banks = {0: [lambda: at_start(ph - 1)], 2: [lambda: in_window(ph - 1)], 5: [lambda: later(ph - 1)]}
+                return steps, banks
 
             for ph in range(1, nph):
                 phase_tiles(ph)
-                hooks = own_hooks(ph)
-                prev = before(ph - 1)
-                for s in (0, 4, 6):
-                    hooks[s] = hooks.get(s, []) + prev[s]
-                run_phase(ph, lambda s: None, hooks)
-            fin_a(fin, O, nph - 1)
-            fin_b(fin, O, nph - 1)
-            fin_c(fin, O, nph - 1)
+                steps, banks = hooks_for(ph)
+                run_phase(ph, lambda s: None, steps, banks)
+
+            ph = nph - 1
+            fin_mean(fin, ph)
+            fin_minmax(O, ph)
+            fin_std(fin, O, ph)
+            fin_amax(O, ph, 0, 2)
+            fin_amax(O, ph, 1, 1)
+            fin_meanout(O, ph)
+            fin_amax(O, ph, 2, 3)
+            fin_store(O, ph)
 
             sc1 = one.tile([P, 4], F32, name="sc1")
             nc.vector.tensor_reduce(out=sc1[:, 0:1], in_=pm[:], axis=AX.X, op=ALU.max)

@@ -20,7 +20,7 @@ F = 1024
 EPS_STD = 1e-5
 FLOPS = 2 * (4096 * 1024 * 1024 + 2 * 128 * 1024 * 1024)
 
-PHASES = ((0, 512, 256), (512, 256, 128), (768, 256, 128))
+PHASES = ((0, 512, 128), (512, 256, 128), (768, 256, 128))
 JC = 4
 SQ_SCALE = (1.0 / 32.0) ** 0.5
 E_BUFS = 5

@@ -20,11 +20,13 @@ F = 1024
 EPS_STD = 1e-5
 FLOPS = 2 * (4096 * 1024 * 1024 + 2 * 128 * 1024 * 1024)
 
-PHASES = ((0, 512, 128), (512, 256, 128), (768, 256, 128))
-JC = 4
+PHASES = ((0, 512, 256), (512, 256, 128), (768, 256, 128))
+XCH = ((0, 4), (4, 12), (16, 16))
 SQ_SCALE = (1.0 / 32.0) ** 0.5
 E_BUFS = 5
 LAZY_COLS = 256
+SQ_COLS = 1024
+LATER = 20
 VCOLS = 2816
 
 
@@ -132,18 +134,19 @@ def tile_gnnlayer_pa_kernel(tc, x, e_enc, W_pre, b_pre, out_0, out_1):
         xs4 = const.tile([P, 2 * P, 4], U8, name="xs4", align_bytes=64)
 
         def x_repeat(c):
-            xr = keep.tile([P, JC, 2, P], I32, name="xr%d" % c, align_bytes=64)
-            xrs = keep.tile([P, JC, 2, P], U8, name="xrs%d" % c, align_bytes=64)
+            j0, jn = XCH[c]
+            xr = keep.tile([P, jn, 2, P], I32, name="xr%d" % c, align_bytes=64)
+            xrs = keep.tile([P, jn, 2, P], U8, name="xrs%d" % c, align_bytes=64)
             codes = xc[:].rearrange("p (g b n) -> p g n b", g=2, b=4)
             words = xs4[:].rearrange("p c r -> p (c r)").bitcast(I32).rearrange("p (g b n) -> p g n b", g=2, b=4)
             for g in range(2):
                 nc.vector.tensor_copy(
                     out=xr[:, :, g, :].rearrange("p j (b i) -> p j b i", b=4),
-                    in_=codes[:, g, c * JC : (c + 1) * JC, :].unsqueeze(3).to_broadcast([P, JC, 4, 32]),
+                    in_=codes[:, g, j0 : j0 + jn, :].unsqueeze(3).to_broadcast([P, jn, 4, 32]),
                 )
                 nc.vector.tensor_copy(
                     out=xrs[:, :, g, :].bitcast(I32).rearrange("p j (b r) -> p j b r", b=4),
-                    in_=words[:, g, c * JC : (c + 1) * JC, :].unsqueeze(3).to_broadcast([P, JC, 4, 8]),
+                    in_=words[:, g, j0 : j0 + jn, :].unsqueeze(3).to_broadcast([P, jn, 4, 8]),
                 )
             st[("xr", c)] = xr
             st[("xrs", c)] = xrs
@@ -159,9 +162,17 @@ def tile_gnnlayer_pa_kernel(tc, x, e_enc, W_pre, b_pre, out_0, out_1):
                 stop=stop,
             )
 
+        def x_chunk(j):
+            c = 0
+            for n in range(len(XCH)):
+                if XCH[n][0] <= j:
+                    c = n
+            return c
+
         def mm_x(ph, j):
             wd = PHASES[ph][1]
-            c, jc = divmod(j, JC)
+            c = x_chunk(j)
+            jc = j - XCH[c][0]
             mb = st[("mb", ph, j)]
             for g in range(2):
                 mx(mb[:], st[("xr", c)][:, jc, g, :], st[("xrs", c)][:, jc, g, :], (1, g, ph), wd, False, g == 1)
@@ -195,28 +206,33 @@ def tile_gnnlayer_pa_kernel(tc, x, e_enc, W_pre, b_pre, out_0, out_1):
                 if nt < wd:
                     nc.vector.tensor_tensor(out=vs[:, nt:wd], in0=mb[:, nt:wd], in1=(m0 if j == 1 else vs)[:, nt:wd], op=ALU.add)
 
+        def group_of(ph):
+            return SQ_COLS // PHASES[ph][1]
+
         def e_sq(ph, j):
             wd = PHASES[ph][1]
-            s, jj = divmod(j, 2)
-            if s == 0:
+            gi, jj = divmod(j, group_of(ph))
+            if gi == 0:
                 dst = st[("acc", ph)]
             else:
                 if jj == 0:
-                    st[("sq", ph, s)] = sqp.tile([P, 2, wd], F32, name="sq", tag="sq")
-                dst = st[("sq", ph, s)]
+                    st[("sq", ph, gi)] = sqp.tile([P, group_of(ph), wd], F32, name="sq", tag="sq")
+                dst = st[("sq", ph, gi)]
             nc.scalar.activation(out=dst[:, jj, :], in_=st[("mb", ph, j)][:], func=ACT.Square, scale=SQ_SCALE)
 
-        def e_acc(ph, s):
-            if 0 < s < NJ // 2 - 1:
+        def e_acc(ph, j):
+            gj = group_of(ph)
+            gi, jj = divmod(j, gj)
+            if jj == gj - 1 and gi > 0 and not (ph == nph - 1 and gi == NJ // gj - 1):
                 acc = st[("acc", ph)]
-                nc.gpsimd.tensor_tensor(out=acc[:], in0=acc[:], in1=st[("sq", ph, s)][:], op=ALU.add)
+                nc.gpsimd.tensor_tensor(out=acc[:], in0=acc[:], in1=st[("sq", ph, gi)][:], op=ALU.add)
 
         def phase_tiles(ph):
             c0, wd, nt = PHASES[ph]
             for nm in ("rmax", "rmin", "vs", "tb", "q"):
                 st[(nm, ph)] = keep.tile([P, wd], F32, name="%s%d" % (nm, ph))
             st[("m0", ph)] = st[("q", ph)]
-            st[("acc", ph)] = keep.tile([P, 2, wd], F32, name="acc%d" % ph)
+            st[("acc", ph)] = keep.tile([P, group_of(ph), wd], F32, name="acc%d" % ph)
             if nt:
                 st[("srcm", ph)] = keep.tile([P, nt], F32, name="srcm%d" % ph)
                 st[("srcs", ph)] = keep.tile([P, nt], F32, name="srcs%d" % ph)
@@ -245,7 +261,9 @@ def tile_gnnlayer_pa_kernel(tc, x, e_enc, W_pre, b_pre, out_0, out_1):
 
         def tgt(ph):
             c0, wd, nt = PHASES[ph]
-            nc.vector.tensor_tensor(out=st[("tb", ph)][:], in0=x_product(0, ph, wd)[:], in1=b_bc[:, c0 : c0 + wd], op=ALU.add)
+            tb = st[("tb", ph)]
+            nc.scalar.copy(out=tb[:], in_=x_product(0, ph, wd)[:])
+            nc.gpsimd.tensor_tensor(out=tb[:], in0=tb[:], in1=b_bc[:, c0 : c0 + wd], op=ALU.add)
 
         def fin_mean(fin, ph):
             c0, wd, nt = PHASES[ph]
@@ -261,31 +279,34 @@ def tile_gnnlayer_pa_kernel(tc, x, e_enc, W_pre, b_pre, out_0, out_1):
             st[("a", ph)] = a
             st[("a2", ph)] = a2
 
-        def fin_q(ph):
+        def fin_q(eng, ph):
             acc = st[("acc", ph)]
-            nc.gpsimd.tensor_tensor(out=st[("q", ph)][:], in0=acc[:, 0, :], in1=acc[:, 1, :], op=ALU.add)
+            if group_of(ph) == 4:
+                eng.tensor_tensor(out=acc[:, 0:2, :], in0=acc[:, 0:2, :], in1=acc[:, 2:4, :], op=ALU.add)
+            eng.tensor_tensor(out=st[("q", ph)][:], in0=acc[:, 0, :], in1=acc[:, 1, :], op=ALU.add)
 
-        def fin_minmax(O, ph):
+        def fin_minmax(eng, O, ph):
             c0, wd, nt = PHASES[ph]
             cols = slice(c0, c0 + wd)
             tb = st[("tb", ph)]
-            nc.vector.tensor_tensor(out=O[:, 2, cols], in0=st[("rmax", ph)][:], in1=tb[:], op=ALU.add)
-            nc.vector.tensor_tensor(out=O[:, 1, cols], in0=st[("rmin", ph)][:], in1=tb[:], op=ALU.add)
+            eng.tensor_tensor(out=O[:, 2, cols], in0=st[("rmax", ph)][:], in1=tb[:], op=ALU.add)
+            eng.tensor_tensor(out=O[:, 1, cols], in0=st[("rmin", ph)][:], in1=tb[:], op=ALU.add)
 
-        def fin_std(fin, O, ph):
+        def fin_std(eng, fin, O, ph):
             c0, wd, nt = PHASES[ph]
             var = fin.tile([P, wd], F32, name="var", tag="var")
-            q = st[("q", ph)]
-            sq = st[("sq", ph, NJ // 2 - 1)]
-            nc.vector.tensor_tensor(out=q[:], in0=q[:], in1=sq[:, 0, :], op=ALU.add)
-            nc.vector.tensor_tensor(out=q[:], in0=q[:], in1=sq[:, 1, :], op=ALU.add)
-            nc.vector.tensor_tensor(out=var[:], in0=q[:], in1=st[("a2", ph)][:], op=ALU.subtract)
+            eng.tensor_tensor(out=var[:], in0=st[("q", ph)][:], in1=st[("a2", ph)][:], op=ALU.subtract)
+            st[("var", ph)] = var
+
+        def fin_sqrt(O, ph):
+            c0, wd, nt = PHASES[ph]
+            var = st[("var", ph)]
             nc.scalar.activation(out=var[:], in_=var[:], func=ACT.Relu)
             nc.scalar.activation(out=O[:, 3, c0 : c0 + wd], in_=var[:], func=ACT.Sqrt, bias=eps[:, 0:1])
 
-        def fin_meanout(O, ph):
+        def fin_meanout(eng, O, ph):
             c0, wd, nt = PHASES[ph]
-            nc.vector.tensor_tensor(out=O[:, 0, c0 : c0 + wd], in0=st[("a", ph)][:], in1=st[("tb", ph)][:], op=ALU.add)
+            eng.tensor_tensor(out=O[:, 0, c0 : c0 + wd], in0=st[("a", ph)][:], in1=st[("tb", ph)][:], op=ALU.add)
 
         def fin_amax(O, ph, n, k):
             c0, wd, nt = PHASES[ph]
@@ -312,12 +333,12 @@ def tile_gnnlayer_pa_kernel(tc, x, e_enc, W_pre, b_pre, out_0, out_1):
                     mm_x(ph, j)
                     e_vec(ph, j)
                     e_sq(ph, j)
+                    e_acc(ph, j)
                     for h in bank_hooks.get(j, ()):
                         h()
-                e_acc(ph, s)
 
         def own_hooks(ph):
-            return {1: [lambda: src_a(ph)], 3: [lambda: src_b(ph)], 5: [lambda: tgt(ph)], NJ // 2 - 1: [lambda: fin_q(ph)]}
+            return {1: [lambda: src_a(ph)], 3: [lambda: src_b(ph)], 5: [lambda: tgt(ph)]}
 
         lazy = [(0, 0, 0), (0, 1, 0)]
         for ph in range(1, nph):
@@ -394,7 +415,7 @@ def tile_gnnlayer_pa_kernel(tc, x, e_enc, W_pre, b_pre, out_0, out_1):
                 if s + 1 < NJ // 2:
                     e_quant(s + 1)
                 if s == 0:
-                    for c in range(1, NJ // JC):
+                    for c in range(1, len(XCH)):
                         x_repeat(c)
 
             run_phase(0, prep0, own_hooks(0), {})
@@ -407,11 +428,10 @@ def tile_gnnlayer_pa_kernel(tc, x, e_enc, W_pre, b_pre, out_0, out_1):
 
             def at_start(ph):
                 fin_mean(fin, ph)
-
-            def in_window(ph):
-                fin_minmax(O, ph)
-                fin_meanout(O, ph)
-                fin_std(fin, O, ph)
+                fin_minmax(nc.gpsimd, O, ph)
+                fin_q(nc.gpsimd, ph)
+                fin_std(nc.gpsimd, fin, O, ph)
+                fin_meanout(nc.gpsimd, O, ph)
 
             def later(ph):
                 for n, k in enumerate((2, 1, 3)):
@@ -420,7 +440,7 @@ def tile_gnnlayer_pa_kernel(tc, x, e_enc, W_pre, b_pre, out_0, out_1):
 
             def hooks_for(ph):
                 steps = own_hooks(ph)
-                banks = {0: [lambda: at_start(ph - 1)], 2: [lambda: in_window(ph - 1)], 5: [lambda: later(ph - 1)]}
+                banks = {0: [lambda: at_start(ph - 1)], LATER - 2: [lambda: fin_sqrt(O, ph - 1)], LATER: [lambda: later(ph - 1)]}
                 return steps, banks
 
             for ph in range(1, nph):
@@ -430,11 +450,15 @@ def tile_gnnlayer_pa_kernel(tc, x, e_enc, W_pre, b_pre, out_0, out_1):
 
             ph = nph - 1
             fin_mean(fin, ph)
-            fin_minmax(O, ph)
-            fin_std(fin, O, ph)
+            acc = st[("acc", ph)]
+            nc.vector.tensor_tensor(out=acc[:], in0=acc[:], in1=st[("sq", ph, NJ // group_of(ph) - 1)][:], op=ALU.add)
+            fin_q(nc.vector, ph)
+            fin_std(nc.vector, fin, O, ph)
+            fin_sqrt(O, ph)
+            fin_minmax(nc.vector, O, ph)
             fin_amax(O, ph, 0, 2)
             fin_amax(O, ph, 1, 1)
-            fin_meanout(O, ph)
+            fin_meanout(nc.vector, O, ph)
             fin_amax(O, ph, 2, 3)
             fin_store(O, ph)
 

@@ -61,6 +61,8 @@ def tile_gnnlayer_pa_kernel(tc, x, e_enc, W_pre, b_pre, out_0, out_1):
             nc.vector.memset(sel[32 * b : 32 * b + 32, 32 * b : 32 * b + 32], 1.0 / NJ)
         eps = const.tile([P, 1], F32, name="eps")
         nc.vector.memset(eps[:], EPS_STD)
+        zero = const.tile([P, 1], F32, name="zero")
+        nc.vector.memset(zero[:], 0.0)
         pm = const.tile([P, 3 * nph], F32, name="pm")
         b_bc = const.tile([P, F], BF16, name="b_bc")
 
@@ -201,31 +203,43 @@ def tile_gnnlayer_pa_kernel(tc, x, e_enc, W_pre, b_pre, out_0, out_1):
                 nc.scalar.copy(out=st[("m0", ph)][:], in_=mb[:])
             else:
                 m0 = st[("m0", ph)]
-                nc.vector.tensor_tensor(out=rmax[:], in0=mb[:], in1=(m0 if j == 1 else rmax)[:], op=ALU.max)
-                nc.vector.tensor_tensor(out=rmin[:], in0=mb[:], in1=(m0 if j == 1 else rmin)[:], op=ALU.min)
                 if nt < wd:
                     nc.vector.tensor_tensor(out=vs[:, nt:wd], in0=mb[:, nt:wd], in1=(m0 if j == 1 else vs)[:, nt:wd], op=ALU.add)
+                nc.vector.tensor_tensor(out=rmax[:], in0=mb[:], in1=(m0 if j == 1 else rmax)[:], op=ALU.max)
+                nc.vector.tensor_tensor(out=rmin[:], in0=mb[:], in1=(m0 if j == 1 else rmin)[:], op=ALU.min)
 
         def group_of(ph):
             return SQ_COLS // PHASES[ph][1]
 
+        def groups_of(ph):
+            g = group_of(ph)
+            if ph < nph - 1:
+                return [(s, g) for s in range(0, NJ, g)]
+            return [(s, g) for s in range(0, NJ, g)]
+
+        def group_at(ph, j):
+            return [(s, n) for s, n in groups_of(ph) if s <= j < s + n][0]
+
         def e_sq(ph, j):
             wd = PHASES[ph][1]
-            gi, jj = divmod(j, group_of(ph))
-            if gi == 0:
+            s, n = group_at(ph, j)
+            if s == 0:
                 dst = st[("acc", ph)]
             else:
-                if jj == 0:
-                    st[("sq", ph, gi)] = sqp.tile([P, group_of(ph), wd], F32, name="sq", tag="sq")
-                dst = st[("sq", ph, gi)]
-            nc.scalar.activation(out=dst[:, jj, :], in_=st[("mb", ph, j)][:], func=ACT.Square, scale=SQ_SCALE)
+                if j == s:
+                    st[("sq", ph, s)] = sqp.tile([P, n, wd], F32, name="sq", tag="sq")
+                dst = st[("sq", ph, s)]
+            nc.scalar.activation(out=dst[:, j - s, :], in_=st[("mb", ph, j)][:], func=ACT.Square, scale=SQ_SCALE)
 
         def e_acc(ph, j):
-            gj = group_of(ph)
-            gi, jj = divmod(j, gj)
-            if jj == gj - 1 and gi > 0 and not (ph == nph - 1 and gi == NJ // gj - 1):
-                acc = st[("acc", ph)]
-                nc.gpsimd.tensor_tensor(out=acc[:], in0=acc[:], in1=st[("sq", ph, gi)][:], op=ALU.add)
+            s, n = group_at(ph, j)
+            if j != s + n - 1 or s == 0 or (ph == nph - 1 and s + n == NJ):
+                return
+            acc = st[("acc", ph)]
+            sq = st[("sq", ph, s)]
+            nc.gpsimd.tensor_tensor(out=acc[:, 0:n, :], in0=acc[:, 0:n, :], in1=sq[:], op=ALU.add)
+            if ph == nph - 1 and s + 2 * n == NJ:
+                fin_q(nc.gpsimd, ph)
 
         def phase_tiles(ph):
             c0, wd, nt = PHASES[ph]
@@ -265,19 +279,29 @@ def tile_gnnlayer_pa_kernel(tc, x, e_enc, W_pre, b_pre, out_0, out_1):
             nc.scalar.copy(out=tb[:], in_=x_product(0, ph, wd)[:])
             nc.gpsimd.tensor_tensor(out=tb[:], in0=tb[:], in1=b_bc[:, c0 : c0 + wd], op=ALU.add)
 
-        def fin_mean(fin, ph):
+        def fin_mean_ts(fin, ph):
             c0, wd, nt = PHASES[ph]
             a = fin.tile([P, wd], F32, name="a", tag="a")
-            a2 = fin.tile([P, wd], F32, name="a2", tag="a2")
+            st[("a", ph)] = a
             if nt:
                 nc.vector.scalar_tensor_tensor(
                     out=a[:, 0:nt], in0=st[("ts", ph)][:], scalar=1.0 / NJ, in1=st[("srcm", ph)][:], op0=ALU.mult, op1=ALU.add
                 )
+
+        def fin_mean_vs(fin, ph):
+            c0, wd, nt = PHASES[ph]
+            a = st[("a", ph)]
+            a2 = fin.tile([P, wd], F32, name="a2", tag="a2")
+            if nt:
+                nc.scalar.activation(out=a2[:, 0:nt], in_=a[:, 0:nt], func=ACT.Square)
             if nt < wd:
+                nc.scalar.activation(out=a2[:, nt:wd], in_=st[("vs", ph)][:, nt:wd], func=ACT.Square, scale=1.0 / NJ)
                 nc.scalar.mul(out=a[:, nt:wd], in_=st[("vs", ph)][:, nt:wd], mul=1.0 / NJ)
-            nc.scalar.activation(out=a2[:], in_=a[:], func=ACT.Square)
-            st[("a", ph)] = a
             st[("a2", ph)] = a2
+
+        def fin_mean(fin, ph):
+            fin_mean_ts(fin, ph)
+            fin_mean_vs(fin, ph)
 
         def fin_q(eng, ph):
             acc = st[("acc", ph)]
@@ -321,7 +345,7 @@ def tile_gnnlayer_pa_kernel(tc, x, e_enc, W_pre, b_pre, out_0, out_1):
         def wd_of(ph):
             return PHASES[ph][1]
 
-        def run_phase(ph, prep, step_hooks, bank_hooks):
+        def run_phase(ph, prep, step_hooks, bank_hooks, early_hooks):
             for s in range(NJ // 2):
                 prep(s)
                 for h in step_hooks.get(s, ()):
@@ -331,6 +355,8 @@ def tile_gnnlayer_pa_kernel(tc, x, e_enc, W_pre, b_pre, out_0, out_1):
                     if not (ph == 0 and s == 0):
                         mm_e(ph, j)
                     mm_x(ph, j)
+                    for h in early_hooks.get(j, ()):
+                        h()
                     e_vec(ph, j)
                     e_sq(ph, j)
                     e_acc(ph, j)
@@ -418,7 +444,7 @@ def tile_gnnlayer_pa_kernel(tc, x, e_enc, W_pre, b_pre, out_0, out_1):
                     for c in range(1, len(XCH)):
                         x_repeat(c)
 
-            run_phase(0, prep0, own_hooks(0), {})
+            run_phase(0, prep0, own_hooks(0), {}, {})
 
         with ExitStack() as c2:
             fin = c2.enter_context(tc.tile_pool(name="fin", bufs=2))
@@ -446,19 +472,28 @@ def tile_gnnlayer_pa_kernel(tc, x, e_enc, W_pre, b_pre, out_0, out_1):
             for ph in range(1, nph):
                 phase_tiles(ph)
                 steps, banks = hooks_for(ph)
-                run_phase(ph, lambda s: None, steps, banks)
+                early = {NJ - 1: [lambda: fin_mean_ts(fin, nph - 1)]} if ph == nph - 1 else {}
+                run_phase(ph, lambda s: None, steps, banks, early)
 
             ph = nph - 1
-            fin_mean(fin, ph)
-            acc = st[("acc", ph)]
-            nc.vector.tensor_tensor(out=acc[:], in0=acc[:], in1=st[("sq", ph, NJ // group_of(ph) - 1)][:], op=ALU.add)
-            fin_q(nc.vector, ph)
-            fin_std(nc.vector, fin, O, ph)
-            fin_sqrt(O, ph)
-            fin_minmax(nc.vector, O, ph)
+            c0, wd, nt = PHASES[ph]
+            cols = slice(c0, c0 + wd)
+            tb = st[("tb", ph)]
+            q = st[("q", ph)]
+            sql = st[("sq", ph, NJ - group_of(ph))]
+            fin_mean_vs(fin, ph)
+            var = fin.tile([P, wd], F32, name="var", tag="var")
+            nc.vector.tensor_tensor(out=sql[:, 0:2, :], in0=sql[:, 0:2, :], in1=sql[:, 2:4, :], op=ALU.add)
+            nc.vector.tensor_tensor(out=O[:, 2, cols], in0=st[("rmax", ph)][:], in1=tb[:], op=ALU.add)
+            nc.vector.tensor_tensor(out=sql[:, 0, :], in0=sql[:, 0, :], in1=sql[:, 1, :], op=ALU.add)
+            nc.vector.tensor_tensor(out=O[:, 1, cols], in0=st[("rmin", ph)][:], in1=tb[:], op=ALU.add)
+            nc.vector.tensor_tensor(out=sql[:, 1, :], in0=sql[:, 0, :], in1=st[("a2", ph)][:], op=ALU.subtract)
             fin_amax(O, ph, 0, 2)
+            nc.vector.tensor_tensor(out=var[:], in0=sql[:, 1, :], in1=q[:], op=ALU.add)
             fin_amax(O, ph, 1, 1)
-            fin_meanout(nc.vector, O, ph)
+            nc.vector.tensor_scalar(out=var[:], in0=var[:], scalar1=0.0, scalar2=EPS_STD, op0=ALU.max, op1=ALU.add)
+            nc.scalar.activation(out=O[:, 3, cols], in_=var[:], func=ACT.Sqrt)
+            fin_meanout(nc.gpsimd, O, ph)
             fin_amax(O, ph, 2, 3)
             fin_store(O, ph)
 
@@ -466,10 +501,12 @@ def tile_gnnlayer_pa_kernel(tc, x, e_enc, W_pre, b_pre, out_0, out_1):
             nc.vector.tensor_reduce(out=sc1[:, 0:1], in_=pm[:], axis=AX.X, op=ALU.max)
             am = ps_x.tile([P, P], F32, name="px", tag="px")
             nc.tensor.transpose(am[:], sc1[:, 0:1].to_broadcast([P, P]), ident[:])
-            nc.vector.tensor_reduce(out=sc1[:, 1:2], in_=am[:], axis=AX.X, op=ALU.max)
+            spread = one.tile([P, P], F32, name="spread")
+            nc.vector.tensor_scalar(
+                out=spread[:], in0=am[:], scalar1=1.0 / 448.0, scalar2=None, op0=ALU.mult, op1=ALU.max, accum_out=sc1[:, 1:2]
+            )
             nc.vector.reciprocal(out=sc1[:, 2:3], in_=sc1[:, 1:2])
-            nc.vector.tensor_scalar(out=sc1[:, 3:4], in0=sc1[:, 2:3], scalar1=448.0, scalar2=None, op0=ALU.mult)
-            fac = sc1[:, 3:4]
+            fac = sc1[:, 2:3]
 
             flat = O[:].rearrange("p k f -> p (k f)")
             vh = VCOLS // 2
@@ -477,11 +514,11 @@ def tile_gnnlayer_pa_kernel(tc, x, e_enc, W_pre, b_pre, out_0, out_1):
             for h in range(2):
                 va = h * vh
                 sa = VCOLS + h * sh
-                tv = fin.tile([P, vh], F32, name="tv", tag="tv")
-                tsc = fin.tile([P, sh], F32, name="tsc", tag="tsc")
-                nc.vector.tensor_scalar(out=tv[:], in0=flat[:, va : va + vh], scalar1=fac, scalar2=None, op0=ALU.mult)
-                nc.scalar.activation(out=tsc[:], in_=flat[:, sa : sa + sh], func=ACT.Copy, scale=fac)
-                nc.vector.tensor_copy(out=o8[:, va : va + vh], in_=tv[:], saturate=False)
-                nc.scalar.copy(out=o8[:, sa : sa + sh], in_=tsc[:], saturate=False)
+                nc.vector.tensor_scalar(
+                    out=o8[:, va : va + vh], in0=flat[:, va : va + vh], scalar1=fac, scalar2=None, op0=ALU.mult, saturate=False
+                )
+                nc.scalar.activation(
+                    out=o8[:, sa : sa + sh], in_=flat[:, sa : sa + sh], func=ACT.Identity, scale=fac, bias=zero[:, 0:1], saturate=False
+                )
                 nc.sync.dma_start(out=o1[:, va : va + vh], in_=o8[:, va : va + vh].bitcast(U8))
                 nc.sync.dma_start(out=o1[:, sa : sa + sh], in_=o8[:, sa : sa + sh].bitcast(U8))

@@ -24,6 +24,7 @@ PHASES = ((0, 512, 256), (512, 256, 128), (768, 256, 128))
 XCH = ((0, 4), (4, 12), (16, 16))
 SQ_SCALE = (1.0 / 32.0) ** 0.5
 E_BUFS = 5
+SQ_BUFS = 4
 LAZY_COLS = 256
 SQ_COLS = 1024
 LATER = 20
@@ -42,7 +43,7 @@ def tile_gnnlayer_pa_kernel(tc, x, e_enc, W_pre, b_pre, out_0, out_1):
         ctx.enter_context(tc.manual_schedule())
         const = ctx.enter_context(tc.tile_pool(name="const", bufs=1))
         keep = ctx.enter_context(tc.tile_pool(name="keep", bufs=1))
-        sqp = ctx.enter_context(tc.tile_pool(name="sqp", bufs=3))
+        sqp = ctx.enter_context(tc.tile_pool(name="sqp", bufs=SQ_BUFS))
         ps_tp = ctx.enter_context(tc.psum_pool(name="ps_tp", bufs=2))
         ps_m = ctx.enter_context(tc.psum_pool(name="ps_m", bufs=4))
         ps_ts = ctx.enter_context(tc.psum_pool(name="ps_ts", bufs=1))
@@ -220,6 +221,10 @@ def tile_gnnlayer_pa_kernel(tc, x, e_enc, W_pre, b_pre, out_0, out_1):
         def group_at(ph, j):
             return [(s, n) for s, n in groups_of(ph) if s <= j < s + n][0]
 
+        def slots(tile, ph):
+            n, wd = group_of(ph), PHASES[ph][1]
+            return tile[:, 0 : n * wd].rearrange("p (n w) -> p n w", n=n)
+
         def e_sq(ph, j):
             wd = PHASES[ph][1]
             s, n = group_at(ph, j)
@@ -227,26 +232,39 @@ def tile_gnnlayer_pa_kernel(tc, x, e_enc, W_pre, b_pre, out_0, out_1):
                 dst = st[("acc", ph)]
             else:
                 if j == s:
-                    st[("sq", ph, s)] = sqp.tile([P, n, wd], F32, name="sq", tag="sq")
+                    st[("sq", ph, s)] = sqp.tile([P, n * wd + 1], F32, name="sq", tag="sq")
                 dst = st[("sq", ph, s)]
-            nc.scalar.activation(out=dst[:, j - s, :], in_=st[("mb", ph, j)][:], func=ACT.Square, scale=SQ_SCALE)
+            nc.scalar.activation(out=slots(dst, ph)[:, j - s, :], in_=st[("mb", ph, j)][:], func=ACT.Square, scale=SQ_SCALE)
+
+        waiting = []
 
         def e_acc(ph, j):
             s, n = group_at(ph, j)
             if j != s + n - 1 or s == 0 or (ph == nph - 1 and s + n == NJ):
                 return
-            acc = st[("acc", ph)]
-            sq = st[("sq", ph, s)]
-            nc.gpsimd.tensor_tensor(out=acc[:, 0:n, :], in0=acc[:, 0:n, :], in1=sq[:], op=ALU.add)
+            if ph == 0:
+                waiting.append(s)
+                return
+            acc = slots(st[("acc", ph)], ph)
+            nc.gpsimd.tensor_tensor(out=acc, in0=acc, in1=slots(st[("sq", ph, s)], ph), op=ALU.add)
             if ph == nph - 1 and s + 2 * n == NJ:
-                fin_q(nc.gpsimd, ph)
+                nc.gpsimd.tensor_tensor(out=acc[:, 0:2, :], in0=acc[:, 0:2, :], in1=acc[:, 2:4, :], op=ALU.add)
+
+        def acc_after_vector():
+            for s in waiting:
+                acc, sq = st[("acc", 0)], st[("sq", 0, s)]
+                n = group_of(0) * PHASES[0][1]
+                nc.vector.memset(sq[:, n : n + 1], 0.0)
+                nc.gpsimd.tensor_tensor(out=acc[:], in0=acc[:], in1=sq[:], op=ALU.add)
+            waiting.clear()
 
         def phase_tiles(ph):
             c0, wd, nt = PHASES[ph]
             for nm in ("rmax", "rmin", "vs", "tb", "q"):
                 st[(nm, ph)] = keep.tile([P, wd], F32, name="%s%d" % (nm, ph))
             st[("m0", ph)] = st[("q", ph)]
-            st[("acc", ph)] = keep.tile([P, group_of(ph), wd], F32, name="acc%d" % ph)
+            st[("acc", ph)] = keep.tile([P, group_of(ph) * wd + 1], F32, name="acc%d" % ph)
+            nc.vector.memset(st[("acc", ph)][:, group_of(ph) * wd : group_of(ph) * wd + 1], 0.0)
             if nt:
                 st[("srcm", ph)] = keep.tile([P, nt], F32, name="srcm%d" % ph)
                 st[("srcs", ph)] = keep.tile([P, nt], F32, name="srcs%d" % ph)
@@ -304,7 +322,7 @@ def tile_gnnlayer_pa_kernel(tc, x, e_enc, W_pre, b_pre, out_0, out_1):
             fin_mean_vs(fin, ph)
 
         def fin_q(eng, ph):
-            acc = st[("acc", ph)]
+            acc = slots(st[("acc", ph)], ph)
             if group_of(ph) == 4:
                 eng.tensor_tensor(out=acc[:, 0:2, :], in0=acc[:, 0:2, :], in1=acc[:, 2:4, :], op=ALU.add)
             eng.tensor_tensor(out=st[("q", ph)][:], in0=acc[:, 0, :], in1=acc[:, 1, :], op=ALU.add)
@@ -364,7 +382,7 @@ def tile_gnnlayer_pa_kernel(tc, x, e_enc, W_pre, b_pre, out_0, out_1):
                         h()
 
         def own_hooks(ph):
-            return {1: [lambda: src_a(ph)], 3: [lambda: src_b(ph)], 5: [lambda: tgt(ph)]}
+            return {1: [lambda: src_a(ph)], 3: [lambda: src_b(ph)], (NJ // 2 - 1 if ph == 0 else 5): [lambda: tgt(ph)]}
 
         lazy = [(0, 0, 0), (0, 1, 0)]
         for ph in range(1, nph):
@@ -440,11 +458,13 @@ def tile_gnnlayer_pa_kernel(tc, x, e_enc, W_pre, b_pre, out_0, out_1):
                     w_quant(u)
                 if s + 1 < NJ // 2:
                     e_quant(s + 1)
+                acc_after_vector()
                 if s == 0:
                     for c in range(1, len(XCH)):
                         x_repeat(c)
 
             run_phase(0, prep0, own_hooks(0), {}, {})
+            acc_after_vector()
 
         with ExitStack() as c2:
             fin = c2.enter_context(tc.tile_pool(name="fin", bufs=2))
@@ -480,20 +500,21 @@ def tile_gnnlayer_pa_kernel(tc, x, e_enc, W_pre, b_pre, out_0, out_1):
             cols = slice(c0, c0 + wd)
             tb = st[("tb", ph)]
             q = st[("q", ph)]
-            sql = st[("sq", ph, NJ - group_of(ph))]
+            sql = slots(st[("sq", ph, NJ - group_of(ph))], ph)
             fin_mean_vs(fin, ph)
             var = fin.tile([P, wd], F32, name="var", tag="var")
+            accl = slots(st[("acc", ph)], ph)
             nc.vector.tensor_tensor(out=sql[:, 0:2, :], in0=sql[:, 0:2, :], in1=sql[:, 2:4, :], op=ALU.add)
             nc.vector.tensor_tensor(out=O[:, 2, cols], in0=st[("rmax", ph)][:], in1=tb[:], op=ALU.add)
-            nc.vector.tensor_tensor(out=sql[:, 0, :], in0=sql[:, 0, :], in1=sql[:, 1, :], op=ALU.add)
+            nc.vector.tensor_tensor(out=sql[:, 0:2, :], in0=sql[:, 0:2, :], in1=accl[:, 0:2, :], op=ALU.add)
             nc.vector.tensor_tensor(out=O[:, 1, cols], in0=st[("rmin", ph)][:], in1=tb[:], op=ALU.add)
-            nc.vector.tensor_tensor(out=sql[:, 1, :], in0=sql[:, 0, :], in1=st[("a2", ph)][:], op=ALU.subtract)
+            nc.vector.tensor_tensor(out=sql[:, 0, :], in0=sql[:, 0, :], in1=sql[:, 1, :], op=ALU.add)
             fin_amax(O, ph, 0, 2)
-            nc.vector.tensor_tensor(out=var[:], in0=sql[:, 1, :], in1=q[:], op=ALU.add)
+            nc.vector.tensor_tensor(out=var[:], in0=sql[:, 0, :], in1=st[("a2", ph)][:], op=ALU.subtract)
             fin_amax(O, ph, 1, 1)
             nc.vector.tensor_scalar(out=var[:], in0=var[:], scalar1=0.0, scalar2=EPS_STD, op0=ALU.max, op1=ALU.add)
             nc.scalar.activation(out=O[:, 3, cols], in_=var[:], func=ACT.Sqrt)
-            fin_meanout(nc.gpsimd, O, ph)
+            fin_meanout(nc.vector, O, ph)
             fin_amax(O, ph, 2, 3)
             fin_store(O, ph)
 

@@ -24,6 +24,8 @@ PHASES = ((0, 512, 256), (512, 256, 128), (768, 256, 128))
 XCH = ((0, 4), (4, 12), (16, 16))
 SQ_SCALE = (1.0 / 32.0) ** 0.5
 E_BUFS = 5
+XSTEP = (0, 0, 0)
+LAZY_FIRST = 1
 SQ_BUFS = 4
 LAZY_COLS = 256
 SQ_COLS = 1024
@@ -389,14 +391,14 @@ def tile_gnnlayer_pa_kernel(tc, x, e_enc, W_pre, b_pre, out_0, out_1):
             lazy.extend([(2, 0, ph), (2, 1, ph), (1, 0, ph), (1, 1, ph), (0, 0, ph), (0, 1, ph)])
 
         lazy_at = {}
-        step, room = 0, LAZY_COLS
+        step, room = LAZY_FIRST, LAZY_COLS
         for u in lazy:
             wd = PHASES[u[2]][1]
             if wd > room and room < LAZY_COLS:
                 step, room = step + 1, LAZY_COLS
             lazy_at.setdefault(step, []).append(u)
             room -= wd
-        assert step <= NJ // 2 - 2
+        assert step <= NJ // 2 - 1
 
         with ExitStack() as c1:
             erp = c1.enter_context(tc.tile_pool(name="erp", bufs=E_BUFS))
@@ -438,7 +440,7 @@ def tile_gnnlayer_pa_kernel(tc, x, e_enc, W_pre, b_pre, out_0, out_1):
             e_load(erp, E_BUFS + 1)
             w_quant((1, 0, 0))
             w_quant((1, 1, 0))
-            for u in lazy_at[0]:
+            for u in lazy_at.get(0, ()):
                 w_load(wrp, u)
             phase_tiles(0)
             mm_e(0, 0)
@@ -458,10 +460,10 @@ def tile_gnnlayer_pa_kernel(tc, x, e_enc, W_pre, b_pre, out_0, out_1):
                     w_quant(u)
                 if s + 1 < NJ // 2:
                     e_quant(s + 1)
-                acc_after_vector()
-                if s == 0:
-                    for c in range(1, len(XCH)):
+                for c in range(1, len(XCH)):
+                    if XSTEP[c] == s:
                         x_repeat(c)
+                acc_after_vector()
 
             run_phase(0, prep0, own_hooks(0), {}, {})
             acc_after_vector()

@@ -24,8 +24,10 @@ PHASES = ((0, 512, 256), (512, 256, 128), (768, 256, 128))
 XCH = ((0, 4), (4, 12), (16, 16))
 SQ_SCALE = (1.0 / 32.0) ** 0.5
 E_BUFS = 5
-XSTEP = (0, 0, 0)
+XSTEP = (0, 0, 2)
+LATE_SUM = (7, 15, 23, 31)
 LAZY_FIRST = 1
+W_LEAD = 2
 SQ_BUFS = 4
 LAZY_COLS = 256
 SQ_COLS = 1024
@@ -190,13 +192,18 @@ def tile_gnnlayer_pa_kernel(tc, x, e_enc, W_pre, b_pre, out_0, out_1):
             for g in range(2):
                 cols = slice((2 * jj + g) * P, (2 * jj + g + 1) * P)
                 mx(mb[:], st[("ec", s)][:, cols], st[("es", s)][:, cols], (2, g, ph), wd, g == 0, False)
-            if nt:
-                for g in range(2):
-                    cols = slice((2 * jj + g) * P, (2 * jj + g + 1) * P)
-                    mx(
-                        st[("ts", ph)][:], st[("ec", s)][:, cols], st[("es", s)][:, cols], (2, g, ph), nt,
-                        j == 0 and g == 0, j == NJ - 1 and g == 1,
-                    )
+            if nt and not (ph == 0 and j in LATE_SUM):
+                mm_ts(ph, j, ph > 0 or not LATE_SUM)
+
+        def mm_ts(ph, j, may_stop):
+            nt = PHASES[ph][2]
+            s, jj = divmod(j, 2)
+            for g in range(2):
+                cols = slice((2 * jj + g) * P, (2 * jj + g + 1) * P)
+                mx(
+                    st[("ts", ph)][:], st[("ec", s)][:, cols], st[("es", s)][:, cols], (2, g, ph), nt,
+                    j == 0 and g == 0, may_stop and g == 1 and j == (LATE_SUM[-1] if ph == 0 and LATE_SUM else NJ - 1),
+                )
 
         def e_vec(ph, j):
             c0, wd, nt = PHASES[ph]
@@ -249,8 +256,6 @@ def tile_gnnlayer_pa_kernel(tc, x, e_enc, W_pre, b_pre, out_0, out_1):
                 return
             acc = slots(st[("acc", ph)], ph)
             nc.gpsimd.tensor_tensor(out=acc, in0=acc, in1=slots(st[("sq", ph, s)], ph), op=ALU.add)
-            if ph == nph - 1 and s + 2 * n == NJ:
-                nc.gpsimd.tensor_tensor(out=acc[:, 0:2, :], in0=acc[:, 0:2, :], in1=acc[:, 2:4, :], op=ALU.add)
 
         def acc_after_vector():
             for s in waiting:
@@ -440,8 +445,9 @@ def tile_gnnlayer_pa_kernel(tc, x, e_enc, W_pre, b_pre, out_0, out_1):
             e_load(erp, E_BUFS + 1)
             w_quant((1, 0, 0))
             w_quant((1, 1, 0))
-            for u in lazy_at.get(0, ()):
-                w_load(wrp, u)
+            for s in range(W_LEAD):
+                for u in lazy_at.get(s, ()):
+                    w_load(wrp, u)
             phase_tiles(0)
             mm_e(0, 0)
             mm_e(0, 1)
@@ -452,7 +458,7 @@ def tile_gnnlayer_pa_kernel(tc, x, e_enc, W_pre, b_pre, out_0, out_1):
                     e_copy(egp, s + 2)
                     if s + 2 + E_BUFS < NJ // 2:
                         e_load(erp, s + 2 + E_BUFS)
-                for u in lazy_at.get(s + 1, ()):
+                for u in lazy_at.get(s + W_LEAD, ()):
                     w_load(wrp, u)
                 for u in lazy_at.get(s, ()):
                     w_interleave(wgp, u, "s")
@@ -475,9 +481,11 @@ def tile_gnnlayer_pa_kernel(tc, x, e_enc, W_pre, b_pre, out_0, out_1):
             o8 = one.tile([P, 4 * F], FP8, name="o8")
 
             def at_start(ph):
-                fin_mean(fin, ph)
                 fin_minmax(nc.gpsimd, O, ph)
                 fin_q(nc.gpsimd, ph)
+
+            def after_sum(ph):
+                fin_mean(fin, ph)
                 fin_std(nc.gpsimd, fin, O, ph)
                 fin_meanout(nc.gpsimd, O, ph)
 
@@ -489,6 +497,10 @@ def tile_gnnlayer_pa_kernel(tc, x, e_enc, W_pre, b_pre, out_0, out_1):
             def hooks_for(ph):
                 steps = own_hooks(ph)
                 banks = {0: [lambda: at_start(ph - 1)], LATER - 2: [lambda: fin_sqrt(O, ph - 1)], LATER: [lambda: later(ph - 1)]}
+                n = len(LATE_SUM) if ph == 1 else 0
+                for k in range(n):
+                    banks.setdefault(k, []).append(lambda k=k: mm_ts(0, LATE_SUM[k], True))
+                banks.setdefault(n, []).append(lambda: after_sum(ph - 1))
                 return steps, banks
 
             for ph in range(1, nph):
@@ -506,9 +518,9 @@ def tile_gnnlayer_pa_kernel(tc, x, e_enc, W_pre, b_pre, out_0, out_1):
             fin_mean_vs(fin, ph)
             var = fin.tile([P, wd], F32, name="var", tag="var")
             accl = slots(st[("acc", ph)], ph)
-            nc.vector.tensor_tensor(out=sql[:, 0:2, :], in0=sql[:, 0:2, :], in1=sql[:, 2:4, :], op=ALU.add)
+            nc.vector.tensor_tensor(out=sql, in0=sql, in1=accl, op=ALU.add)
             nc.vector.tensor_tensor(out=O[:, 2, cols], in0=st[("rmax", ph)][:], in1=tb[:], op=ALU.add)
-            nc.vector.tensor_tensor(out=sql[:, 0:2, :], in0=sql[:, 0:2, :], in1=accl[:, 0:2, :], op=ALU.add)
+            nc.vector.tensor_tensor(out=sql[:, 0:2, :], in0=sql[:, 0:2, :], in1=sql[:, 2:4, :], op=ALU.add)
             nc.vector.tensor_tensor(out=O[:, 1, cols], in0=st[("rmin", ph)][:], in1=tb[:], op=ALU.add)
             nc.vector.tensor_tensor(out=sql[:, 0, :], in0=sql[:, 0, :], in1=sql[:, 1, :], op=ALU.add)
             fin_amax(O, ph, 0, 2)

@@ -28,6 +28,7 @@ XSTEP = (0, 0, 2)
 LATE_SUM = (7, 15, 23, 31)
 LAZY_FIRST = 1
 W_LEAD = 2
+N_WARM = 6
 SQ_BUFS = 4
 LAZY_COLS = 256
 SQ_COLS = 1024
@@ -68,6 +69,8 @@ def tile_gnnlayer_pa_kernel(tc, x, e_enc, W_pre, b_pre, out_0, out_1):
         nc.vector.memset(eps[:], EPS_STD)
         zero = const.tile([P, 1], F32, name="zero")
         nc.vector.memset(zero[:], 0.0)
+        zeros = const.tile([P, 512], BF16, name="zeros")
+        nc.gpsimd.memset(zeros[:], 0.0)
         pm = const.tile([P, 3 * nph], F32, name="pm")
         b_bc = const.tile([P, F], BF16, name="b_bc")
 
@@ -428,6 +431,9 @@ def tile_gnnlayer_pa_kernel(tc, x, e_enc, W_pre, b_pre, out_0, out_1):
             tpx = transpose4(x_sb[:].bitcast(F32), 0)
             nc.scalar.copy(out=xg[:].bitcast(F32), in_=tpx[:].rearrange("p g u r -> p g r u"))
             e_transpose(0)
+            warm_out = ps_x.tile([P, 512], F32, name="px", tag="px")
+            for n in range(N_WARM):
+                nc.tensor.matmul(out=warm_out[:], lhsT=zeros[:, 0:P], rhs=zeros[:], start=True, stop=True)
             e_copy(egp, 0)
             e_load(erp, E_BUFS)
             w_interleave(wgp, (2, 1, 0), "s")

@@ -29,6 +29,7 @@ LATE_SUM = (7, 15, 23, 31)
 LAZY_FIRST = 1
 W_LEAD = 2
 N_WARM = 6
+BIAS_STEP = 8
 SQ_BUFS = 4
 LAZY_COLS = 256
 SQ_COLS = 1024
@@ -422,7 +423,6 @@ def tile_gnnlayer_pa_kernel(tc, x, e_enc, W_pre, b_pre, out_0, out_1):
             w_load(wrp, (1, 1, 0))
             e_load(erp, 1)
             e_load(erp, 2)
-            nc.sync.dma_start(out=b_bc[:], in_=b_pre.partition_broadcast(P))
             for s in range(3, E_BUFS):
                 e_load(erp, s)
 
@@ -466,6 +466,8 @@ def tile_gnnlayer_pa_kernel(tc, x, e_enc, W_pre, b_pre, out_0, out_1):
                         e_load(erp, s + 2 + E_BUFS)
                 for u in lazy_at.get(s + W_LEAD, ()):
                     w_load(wrp, u)
+                if s == BIAS_STEP:
+                    nc.sync.dma_start(out=b_bc[:], in_=b_pre.partition_broadcast(P))
                 for u in lazy_at.get(s, ()):
                     w_interleave(wgp, u, "s")
                 for u in lazy_at.get(s - 1, ()):

@@ -30,6 +30,7 @@ LAZY_FIRST = 1
 W_LEAD = 2
 N_WARM = 6
 BIAS_STEP = 8
+BETWEEN = 1
 SQ_BUFS = 4
 LAZY_COLS = 256
 SQ_COLS = 1024
@@ -87,13 +88,12 @@ def tile_gnnlayer_pa_kernel(tc, x, e_enc, W_pre, b_pre, out_0, out_1):
             wd = PHASES[u[2]][1]
             raw = st[("wraw", u)]
             grp = pool.tile([P, wd, 4], BF16, name="wgrp", tag="wgrp", align_bytes=64)
-            src = raw[:].rearrange("p t f -> p f t")
+            src = raw[:].rearrange("p t (c i) -> p c t i", i=4)
+            dst = grp[:].rearrange("p (c i) t -> p c t i", i=4)
             if eng == "v":
-                nc.vector.tensor_copy(out=grp[:], in_=src)
-            elif eng == "s":
-                nc.scalar.copy(out=grp[:], in_=src)
+                nc.vector.tensor_copy(out=dst, in_=src)
             else:
-                nc.gpsimd.tensor_scalar(out=grp[:], in0=src, scalar1=1.0, scalar2=0.0, op0=ALU.mult, op1=ALU.add)
+                nc.scalar.copy(out=dst, in_=src)
             st[("wgrp", u)] = grp
 
         def w_quant(u):
@@ -250,6 +250,7 @@ def tile_gnnlayer_pa_kernel(tc, x, e_enc, W_pre, b_pre, out_0, out_1):
             nc.scalar.activation(out=slots(dst, ph)[:, j - s, :], in_=st[("mb", ph, j)][:], func=ACT.Square, scale=SQ_SCALE)
 
         waiting = []
+        between = []
 
         def e_acc(ph, j):
             s, n = group_at(ph, j)
@@ -260,6 +261,11 @@ def tile_gnnlayer_pa_kernel(tc, x, e_enc, W_pre, b_pre, out_0, out_1):
                 return
             acc = slots(st[("acc", ph)], ph)
             nc.gpsimd.tensor_tensor(out=acc, in0=acc, in1=slots(st[("sq", ph, s)], ph), op=ALU.add)
+            for h in between[0:BETWEEN]:
+                h()
+            rest = between[BETWEEN:]
+            between.clear()
+            between.extend(rest)
 
         def acc_after_vector():
             for s in waiting:
@@ -489,13 +495,23 @@ def tile_gnnlayer_pa_kernel(tc, x, e_enc, W_pre, b_pre, out_0, out_1):
             o8 = one.tile([P, 4 * F], FP8, name="o8")
 
             def at_start(ph):
-                fin_minmax(nc.gpsimd, O, ph)
                 fin_q(nc.gpsimd, ph)
 
             def after_sum(ph):
                 fin_mean(fin, ph)
                 fin_std(nc.gpsimd, fin, O, ph)
-                fin_meanout(nc.gpsimd, O, ph)
+                c0, wd, nt = PHASES[ph]
+                cols = slice(c0, c0 + wd)
+                tb = st[("tb", ph)]
+                between.extend([
+                    lambda: nc.gpsimd.tensor_tensor(out=O[:, 2, cols], in0=st[("rmax", ph)][:], in1=tb[:], op=ALU.add),
+                    lambda: nc.gpsimd.tensor_tensor(out=O[:, 1, cols], in0=st[("rmin", ph)][:], in1=tb[:], op=ALU.add),
+                    lambda: fin_meanout(nc.gpsimd, O, ph),
+                ])
+                if BETWEEN == 0:
+                    for h in between:
+                        h()
+                    between.clear()
 
             def later(ph):
                 for n, k in enumerate((2, 1, 3)):

@@ -316,7 +316,7 @@ def tile_gnnlayer_pa_kernel(tc, x, e_enc, W_pre, b_pre, out_0, out_1):
 
         def fin_mean_ts(fin, ph):
             c0, wd, nt = PHASES[ph]
-            a = fin.tile([P, wd], F32, name="a", tag="a")
+            a = st["one"].tile([P, wd], F32, name="a%d" % ph)
             st[("a", ph)] = a
             if nt:
                 nc.vector.scalar_tensor_tensor(
@@ -375,7 +375,7 @@ def tile_gnnlayer_pa_kernel(tc, x, e_enc, W_pre, b_pre, out_0, out_1):
 
         def fin_store(O, ph):
             c0, wd, nt = PHASES[ph]
-            nc.sync.dma_start(out=o0[:, :, c0 : c0 + wd], in_=O[:, :, c0 : c0 + wd])
+            nc.sync.dma_start(out=o0[:, 1:4, c0 : c0 + wd], in_=O[:, 1:4, c0 : c0 + wd])
 
         def wd_of(ph):
             return PHASES[ph][1]
@@ -491,6 +491,7 @@ def tile_gnnlayer_pa_kernel(tc, x, e_enc, W_pre, b_pre, out_0, out_1):
         with ExitStack() as c2:
             fin = c2.enter_context(tc.tile_pool(name="fin", bufs=2))
             one = c2.enter_context(tc.tile_pool(name="one", bufs=1))
+            st["one"] = one
             O = one.tile([P, 4, F], F32, name="O")
             o8 = one.tile([P, 4 * F], FP8, name="o8")
 
@@ -506,7 +507,6 @@ def tile_gnnlayer_pa_kernel(tc, x, e_enc, W_pre, b_pre, out_0, out_1):
                 between.extend([
                     lambda: nc.gpsimd.tensor_tensor(out=O[:, 2, cols], in0=st[("rmax", ph)][:], in1=tb[:], op=ALU.add),
                     lambda: nc.gpsimd.tensor_tensor(out=O[:, 1, cols], in0=st[("rmin", ph)][:], in1=tb[:], op=ALU.add),
-                    lambda: fin_meanout(nc.gpsimd, O, ph),
                 ])
                 if BETWEEN == 0:
                     for h in between:
@@ -552,14 +552,18 @@ def tile_gnnlayer_pa_kernel(tc, x, e_enc, W_pre, b_pre, out_0, out_1):
             fin_amax(O, ph, 1, 1)
             nc.vector.tensor_scalar(out=var[:], in0=var[:], scalar1=0.0, scalar2=EPS_STD, op0=ALU.max, op1=ALU.add)
             nc.scalar.activation(out=O[:, 3, cols], in_=var[:], func=ACT.Sqrt)
-            fin_meanout(nc.vector, O, ph)
+            for p in range(1, nph):
+                fin_meanout(nc.vector, O, p)
             fin_amax(O, ph, 2, 3)
             fin_store(O, ph)
+            nc.sync.dma_start(out=o0[:, 0, PHASES[1][0] : F], in_=O[:, 0, PHASES[1][0] : F])
 
             sc1 = one.tile([P, 4], F32, name="sc1")
             nc.vector.tensor_reduce(out=sc1[:, 0:1], in_=pm[:], axis=AX.X, op=ALU.max)
             am = ps_x.tile([P, P], F32, name="px", tag="px")
             nc.tensor.transpose(am[:], sc1[:, 0:1].to_broadcast([P, P]), ident[:])
+            fin_meanout(nc.vector, O, 0)
+            nc.sync.dma_start(out=o0[:, 0, 0 : PHASES[0][1]], in_=O[:, 0, 0 : PHASES[0][1]])
             spread = one.tile([P, P], F32, name="spread")
             nc.vector.tensor_scalar(
                 out=spread[:], in0=am[:], scalar1=1.0 / 448.0, scalar2=None, op0=ALU.mult, op1=ALU.max, accum_out=sc1[:, 1:2]

@@ -73,7 +73,7 @@ def tile_gnnlayer_pa_kernel(tc, x, e_enc, W_pre, b_pre, out_0, out_1):
         nc.vector.memset(zero[:], 0.0)
         zeros = const.tile([P, 512], BF16, name="zeros")
         nc.gpsimd.memset(zeros[:], 0.0)
-        pm = const.tile([P, 3 * nph], F32, name="pm")
+        pm = const.tile([P, 3 * nph - 1], F32, name="pm")
         b_bc = const.tile([P, F], BF16, name="b_bc")
 
         def w_load(pool, u):
@@ -196,7 +196,7 @@ def tile_gnnlayer_pa_kernel(tc, x, e_enc, W_pre, b_pre, out_0, out_1):
             for g in range(2):
                 cols = slice((2 * jj + g) * P, (2 * jj + g + 1) * P)
                 mx(mb[:], st[("ec", s)][:, cols], st[("es", s)][:, cols], (2, g, ph), wd, g == 0, False)
-            if nt and not (ph == 0 and j in LATE_SUM):
+            if nt and not (ph == 0 and j in LATE_SUM) and not (ph == nph - 1 and j == NJ - 1):
                 mm_ts(ph, j, ph > 0 or not LATE_SUM)
 
         def mm_ts(ph, j, may_stop):
@@ -390,6 +390,8 @@ def tile_gnnlayer_pa_kernel(tc, x, e_enc, W_pre, b_pre, out_0, out_1):
                     if not (ph == 0 and s == 0):
                         mm_e(ph, j)
                     mm_x(ph, j)
+                    if ph == nph - 1 and j == NJ - 1:
+                        mm_ts(ph, j, True)
                     for h in early_hooks.get(j, ()):
                         h()
                     e_vec(ph, j)
@@ -530,8 +532,7 @@ def tile_gnnlayer_pa_kernel(tc, x, e_enc, W_pre, b_pre, out_0, out_1):
             for ph in range(1, nph):
                 phase_tiles(ph)
                 steps, banks = hooks_for(ph)
-                early = {NJ - 1: [lambda: fin_mean_ts(fin, nph - 1)]} if ph == nph - 1 else {}
-                run_phase(ph, lambda s: None, steps, banks, early)
+                run_phase(ph, lambda s: None, steps, banks, {})
 
             ph = nph - 1
             c0, wd, nt = PHASES[ph]
@@ -539,27 +540,30 @@ def tile_gnnlayer_pa_kernel(tc, x, e_enc, W_pre, b_pre, out_0, out_1):
             tb = st[("tb", ph)]
             q = st[("q", ph)]
             sql = slots(st[("sq", ph, NJ - group_of(ph))], ph)
-            fin_mean_vs(fin, ph)
             var = fin.tile([P, wd], F32, name="var", tag="var")
+            sd = one.tile([P, wd + 1], F32, name="sd")
+            sc1 = one.tile([P, 4], F32, name="sc1")
             accl = slots(st[("acc", ph)], ph)
-            nc.vector.tensor_tensor(out=sql, in0=sql, in1=accl, op=ALU.add)
             nc.vector.tensor_tensor(out=O[:, 2, cols], in0=st[("rmax", ph)][:], in1=tb[:], op=ALU.add)
-            nc.vector.tensor_tensor(out=sql[:, 0:2, :], in0=sql[:, 0:2, :], in1=sql[:, 2:4, :], op=ALU.add)
             nc.vector.tensor_tensor(out=O[:, 1, cols], in0=st[("rmin", ph)][:], in1=tb[:], op=ALU.add)
-            nc.vector.tensor_tensor(out=sql[:, 0, :], in0=sql[:, 0, :], in1=sql[:, 1, :], op=ALU.add)
+            nc.vector.tensor_tensor(out=sql, in0=sql, in1=accl, op=ALU.add)
+            fin_mean_ts(fin, ph)
+            fin_mean_vs(fin, ph)
+            nc.vector.tensor_tensor(out=sql[:, 0:2, :], in0=sql[:, 0:2, :], in1=sql[:, 2:4, :], op=ALU.add)
             fin_amax(O, ph, 0, 2)
-            nc.vector.tensor_tensor(out=var[:], in0=sql[:, 0, :], in1=st[("a2", ph)][:], op=ALU.subtract)
+            nc.vector.tensor_tensor(out=sql[:, 0, :], in0=sql[:, 0, :], in1=sql[:, 1, :], op=ALU.add)
             fin_amax(O, ph, 1, 1)
+            nc.vector.tensor_tensor(out=var[:], in0=sql[:, 0, :], in1=st[("a2", ph)][:], op=ALU.subtract)
+            nc.vector.tensor_reduce(out=sd[:, wd : wd + 1], in_=pm[:], axis=AX.X, op=ALU.max)
             nc.vector.tensor_scalar(out=var[:], in0=var[:], scalar1=0.0, scalar2=EPS_STD, op0=ALU.max, op1=ALU.add)
-            nc.scalar.activation(out=O[:, 3, cols], in_=var[:], func=ACT.Sqrt)
+            nc.scalar.activation(out=sd[:, 0:wd], in_=var[:], func=ACT.Sqrt)
+            nc.scalar.copy(out=O[:, 3, cols], in_=sd[:, 0:wd])
             for p in range(1, nph):
                 fin_meanout(nc.vector, O, p)
-            fin_amax(O, ph, 2, 3)
+
+            nc.vector.tensor_reduce(out=sc1[:, 0:1], in_=sd[:], axis=AX.X, op=ALU.max)
             fin_store(O, ph)
             nc.sync.dma_start(out=o0[:, 0, PHASES[1][0] : F], in_=O[:, 0, PHASES[1][0] : F])
-
-            sc1 = one.tile([P, 4], F32, name="sc1")
-            nc.vector.tensor_reduce(out=sc1[:, 0:1], in_=pm[:], axis=AX.X, op=ALU.max)
             am = ps_x.tile([P, P], F32, name="px", tag="px")
             nc.tensor.transpose(am[:], sc1[:, 0:1].to_broadcast([P, P]), ident[:])
             fin_meanout(nc.vector, O, 0)

@@ -26,7 +26,7 @@ SQ_SCALE = (1.0 / 32.0) ** 0.5
 E_BUFS = 5
 XSTEP = (0, 0, 2)
 LATE_SUM = (7, 15, 23, 31)
-LAZY_FIRST = 1
+LAZY_FIRST = 2
 W_LEAD = 2
 N_WARM = 6
 BIAS_STEP = 8
@@ -408,14 +408,14 @@ def tile_gnnlayer_pa_kernel(tc, x, e_enc, W_pre, b_pre, out_0, out_1):
             lazy.extend([(2, 0, ph), (2, 1, ph), (1, 0, ph), (1, 1, ph), (0, 0, ph), (0, 1, ph)])
 
         lazy_at = {}
-        step, room = LAZY_FIRST, LAZY_COLS
-        for u in lazy:
-            wd = PHASES[u[2]][1]
-            if wd > room and room < LAZY_COLS:
-                step, room = step + 1, LAZY_COLS
-            lazy_at.setdefault(step, []).append(u)
-            room -= wd
-        assert step <= NJ // 2 - 1
+        lazy_steps = list(range(LAZY_FIRST, NJ // 2 - 1))
+        double = len(lazy) - len(lazy_steps)
+        k = 0
+        for n, step in enumerate(lazy_steps):
+            take = 2 if n >= len(lazy_steps) - double else 1
+            lazy_at[step] = lazy[k : k + take]
+            k += take
+        assert k == len(lazy)
 
         with ExitStack() as c1:
             erp = c1.enter_context(tc.tile_pool(name="erp", bufs=E_BUFS))

@@ -546,6 +546,7 @@ def tile_gnnlayer_pa_kernel(tc, x, e_enc, W_pre, b_pre, out_0, out_1):
             accl = slots(st[("acc", ph)], ph)
             nc.vector.tensor_tensor(out=O[:, 2, cols], in0=st[("rmax", ph)][:], in1=tb[:], op=ALU.add)
             nc.vector.tensor_tensor(out=O[:, 1, cols], in0=st[("rmin", ph)][:], in1=tb[:], op=ALU.add)
+            nc.sync.dma_start(out=o0[:, 1:3, cols], in_=O[:, 1:3, cols])
             nc.vector.tensor_tensor(out=sql, in0=sql, in1=accl, op=ALU.add)
             fin_mean_ts(fin, ph)
             fin_mean_vs(fin, ph)
@@ -562,8 +563,8 @@ def tile_gnnlayer_pa_kernel(tc, x, e_enc, W_pre, b_pre, out_0, out_1):
                 fin_meanout(nc.vector, O, p)
 
             nc.vector.tensor_reduce(out=sc1[:, 0:1], in_=sd[:], axis=AX.X, op=ALU.max)
-            fin_store(O, ph)
             nc.sync.dma_start(out=o0[:, 0, PHASES[1][0] : F], in_=O[:, 0, PHASES[1][0] : F])
+            nc.sync.dma_start(out=o0[:, 3, cols], in_=O[:, 3, cols])
             am = ps_x.tile([P, P], F32, name="px", tag="px")
             nc.tensor.transpose(am[:], sc1[:, 0:1].to_broadcast([P, P]), ident[:])
             fin_meanout(nc.vector, O, 0)

from contextlib import ExitStack

import concourse.mybir as mybir
from concourse.masks import make_identity

F32 = mybir.dt.float32
BF16 = mybir.dt.bfloat16
I32 = mybir.dt.int32
U8 = mybir.dt.uint8
FP8X4 = mybir.dt.float8_e4m3fn_x4
FP8 = mybir.dt.float8_e4m3fn
ALU = mybir.AluOpType
ACT = mybir.ActivationFunctionType
AX = mybir.AxisListType

P = 128
NJ = 32
C = 1024
F = 1024
EPS_STD = 1e-5
FLOPS = 2 * (4096 * 1024 * 1024 + 2 * 128 * 1024 * 1024)

PHASES = ((0, 512, 256), (512, 256, 128), (768, 256, 128))
XCH = ((0, 4), (4, 12), (16, 16))
SQ_SCALE = (1.0 / 32.0) ** 0.5
E_BUFS = 5
XSTEP = (0, 0, 2)
LATE_SUM = (7, 15, 23, 31)
LAZY_FIRST = 2
W_LEAD = 2
N_WARM = 6
BIAS_STEP = 8
BETWEEN = 1
SQ_BUFS = 4
LAZY_COLS = 256
SQ_COLS = 1024
LATER = 20
VCOLS = 2816


def tile_gnnlayer_pa_kernel(tc, x, e_enc, W_pre, b_pre, out_0, out_1):
    nc = tc.nc
    nph = len(PHASES)
    x_rows = x.rearrange("b n c -> (b n) c")
    e_rows = e_enc.rearrange("b i j c -> (b i) j c")
    o0 = out_0.rearrange("b i (k f) -> (b i) k f", k=4)
    o1 = out_1.rearrange("b i f -> (b i) f")

    with ExitStack() as ctx:
        ctx.enter_context(tc.manual_schedule())
        const = ctx.enter_context(tc.tile_pool(name="const", bufs=1))
        keep = ctx.enter_context(tc.tile_pool(name="keep", bufs=1))
        sqp = ctx.enter_context(tc.tile_pool(name="sqp", bufs=SQ_BUFS))
        ps_tp = ctx.enter_context(tc.psum_pool(name="ps_tp", bufs=2))
        ps_m = ctx.enter_context(tc.psum_pool(name="ps_m", bufs=4))
        ps_ts = ctx.enter_context(tc.psum_pool(name="ps_ts", bufs=1))
        ps_x = ctx.enter_context(tc.psum_pool(name="ps_x", bufs=1))

        st = {}

        ident = const.tile([P, P], F32, name="ident")
        make_identity(nc, ident[:])
        warm = const.tile([P, 2], F32, name="warm")
        nc.vector.memset(warm[:], 1.0)
        nc.scalar.activation(out=warm[:, 1:2], in_=warm[:, 0:1], func=ACT.Sqrt)
        sel = const.tile([P, P], F32, name="sel")
        nc.vector.memset(sel[:], 0.0)
        for b in range(4):
            nc.vector.memset(sel[32 * b : 32 * b + 32, 32 * b : 32 * b + 32], 1.0 / NJ)
        eps = const.tile([P, 1], F32, name="eps")
        nc.vector.memset(eps[:], EPS_STD)
        zero = const.tile([P, 1], F32, name="zero")
        nc.vector.memset(zero[:], 0.0)
        zeros = const.tile([P, 512], BF16, name="zeros")
        nc.gpsimd.memset(zeros[:], 0.0)
        pm = const.tile([P, 3 * nph - 1], F32, name="pm")
        b_bc = const.tile([P, F], BF16, name="b_bc")

        def w_load(pool, u):
            w, g, ph = u
            c0, wd, nt = PHASES[ph]
            raw = pool.tile([P, 4, wd], BF16, name="wraw", tag="wraw")
            r0 = w * C + g * 512
            nc.sync.dma_start(out=raw[:], in_=W_pre[r0 : r0 + 512, c0 : c0 + wd].rearrange("(p t) f -> p t f", t=4))
            st[("wraw", u)] = raw

        def w_interleave(pool, u, eng):
            wd = PHASES[u[2]][1]
            raw = st[("wraw", u)]
            grp = pool.tile([P, wd, 4], BF16, name="wgrp", tag="wgrp", align_bytes=64)
            src = raw[:].rearrange("p t (c i) -> p c t i", i=4)
            dst = grp[:].rearrange("p (c i) t -> p c t i", i=4)
            if eng == "v":
                nc.vector.tensor_copy(out=dst, in_=src)
            else:
                nc.scalar.copy(out=dst, in_=src)
            st[("wgrp", u)] = grp

        def w_quant(u):
            wd = PHASES[u[2]][1]
            grp = st[("wgrp", u)]
            wc = keep.tile([P, wd], I32, name="wc%d%d%d" % u, align_bytes=64)
            ws = keep.tile([P, wd], U8, name="ws%d%d%d" % u, align_bytes=64)
            nc.vector.quantize_mx(out=wc[:].bitcast(FP8X4), scales=ws[:], in_=grp[:].rearrange("p f t -> p (f t)"))
            st[("wc", u)] = wc
            st[("ws", u)] = ws

        def e_load(pool, s):
            er = pool.tile([P, 2, C], BF16, name="er", tag="er")
            nc.sync.dma_start(out=er[:], in_=e_rows[:, 2 * s : 2 * s + 2, :])
            st[("er", s)] = er

        def transpose4(words, base):
            tp = ps_tp.tile([P, 2, 2, P], F32, name="tp", tag="tp")
            for g in range(2):
                for u in range(2):
                    lo = base + 256 * g
                    nc.tensor.transpose(tp[:, g, u, :], words[:, lo + u : lo + 256 : 2], ident[:])
            return tp

        def e_transpose(s):
            words = st[("er", s)][:].rearrange("p j c -> p (j c)").bitcast(F32)
            for jj in range(2):
                st[("tp", s, jj)] = transpose4(words, 512 * jj)

        def e_copy(pool, s):
            eg = pool.tile([P, 2, 2, P, 4], BF16, name="eg", tag="eg", align_bytes=64)
            for jj in range(2):
                nc.scalar.copy(out=eg[:, jj].bitcast(F32), in_=st[("tp", s, jj)][:].rearrange("p g u r -> p g r u"))
            st[("eg", s)] = eg

        def e_quant(s):
            ec = keep.tile([P, 4 * P], I32, name="ec%d" % s, align_bytes=64)
            es = keep.tile([P, 4 * P], U8, name="es%d" % s, align_bytes=64)
            nc.vector.quantize_mx(
                out=ec[:].bitcast(FP8X4), scales=es[:], in_=st[("eg", s)][:].rearrange("p j g r t -> p (j g r t)")
            )
            st[("ec", s)] = ec
            st[("es", s)] = es

        x_sb = const.tile([P, C], BF16, name="x_sb")
        xg = const.tile([P, 2, P, 4], BF16, name="xg", align_bytes=64)
        xc = const.tile([P, 2 * P], I32, name="xc", align_bytes=64)
        xs = const.tile([P, 2 * P], U8, name="xs", align_bytes=64)
        xs4 = const.tile([P, 2 * P, 4], U8, name="xs4", align_bytes=64)

        def x_repeat(c):
            j0, jn = XCH[c]
            xr = keep.tile([P, jn, 2, P], I32, name="xr%d" % c, align_bytes=64)
            xrs = keep.tile([P, jn, 2, P], U8, name="xrs%d" % c, align_bytes=64)
            codes = xc[:].rearrange("p (g b n) -> p g n b", g=2, b=4)
            words = xs4[:].rearrange("p c r -> p (c r)").bitcast(I32).rearrange("p (g b n) -> p g n b", g=2, b=4)
            for g in range(2):
                nc.vector.tensor_copy(
                    out=xr[:, :, g, :].rearrange("p j (b i) -> p j b i", b=4),
                    in_=codes[:, g, j0 : j0 + jn, :].unsqueeze(3).to_broadcast([P, jn, 4, 32]),
                )
                nc.vector.tensor_copy(
                    out=xrs[:, :, g, :].bitcast(I32).rearrange("p j (b r) -> p j b r", b=4),
                    in_=words[:, g, j0 : j0 + jn, :].unsqueeze(3).to_broadcast([P, jn, 4, 8]),
                )
            st[("xr", c)] = xr
            st[("xrs", c)] = xrs

        def mx(out, lhsT, lhsT_scale, u, n, start, stop):
            nc.tensor.matmul_mx(
                out=out,
                lhsT=lhsT.bitcast(FP8X4),
                lhsT_scale=lhsT_scale,
                rhs=st[("wc", u)][:, 0:n].bitcast(FP8X4),
                rhs_scale=st[("ws", u)][:, 0:n],
                start=start,
                stop=stop,
            )

        def x_chunk(j):
            c = 0
            for n in range(len(XCH)):
                if XCH[n][0] <= j:
                    c = n
            return c

        def mm_x(ph, j):
            wd = PHASES[ph][1]
            c = x_chunk(j)
            jc = j - XCH[c][0]
            mb = st[("mb", ph, j)]
            for g in range(2):
                mx(mb[:], st[("xr", c)][:, jc, g, :], st[("xrs", c)][:, jc, g, :], (1, g, ph), wd, False, g == 1)

        def mm_e(ph, j):
            c0, wd, nt = PHASES[ph]
            s, jj = divmod(j, 2)
            mb = ps_m.tile([P, wd], F32, name="mb", tag="mb")
            st[("mb", ph, j)] = mb
            for g in range(2):
                cols = slice((2 * jj + g) * P, (2 * jj + g + 1) * P)
                mx(mb[:], st[("ec", s)][:, cols], st[("es", s)][:, cols], (2, g, ph), wd, g == 0, False)
            if nt and not (ph == 0 and j in LATE_SUM) and not (ph == nph - 1 and j == NJ - 1):
                mm_ts(ph, j, ph > 0 or not LATE_SUM)

        def mm_ts(ph, j, may_stop):
            nt = PHASES[ph][2]
            s, jj = divmod(j, 2)
            for g in range(2):
                cols = slice((2 * jj + g) * P, (2 * jj + g + 1) * P)
                mx(
                    st[("ts", ph)][:], st[("ec", s)][:, cols], st[("es", s)][:, cols], (2, g, ph), nt,
                    j == 0 and g == 0, may_stop and g == 1 and j == (LATE_SUM[-1] if ph == 0 and LATE_SUM else NJ - 1),
                )

        def e_vec(ph, j):
            c0, wd, nt = PHASES[ph]
            mb = st[("mb", ph, j)]
            rmax, rmin, vs = st[("rmax", ph)], st[("rmin", ph)], st[("vs", ph)]
            if j == 0:
                nc.scalar.copy(out=st[("m0", ph)][:], in_=mb[:])
            else:
                m0 = st[("m0", ph)]
                if nt < wd:
                    nc.vector.tensor_tensor(out=vs[:, nt:wd], in0=mb[:, nt:wd], in1=(m0 if j == 1 else vs)[:, nt:wd], op=ALU.add)
                nc.vector.tensor_tensor(out=rmax[:], in0=mb[:], in1=(m0 if j == 1 else rmax)[:], op=ALU.max)
                nc.vector.tensor_tensor(out=rmin[:], in0=mb[:], in1=(m0 if j == 1 else rmin)[:], op=ALU.min)

        def group_of(ph):
            return SQ_COLS // PHASES[ph][1]

        def groups_of(ph):
            g = group_of(ph)
            if ph < nph - 1:
                return [(s, g) for s in range(0, NJ, g)]
            return [(s, g) for s in range(0, NJ, g)]

        def group_at(ph, j):
            return [(s, n) for s, n in groups_of(ph) if s <= j < s + n][0]

        def slots(tile, ph):
            n, wd = group_of(ph), PHASES[ph][1]
            return tile[:, 0 : n * wd].rearrange("p (n w) -> p n w", n=n)

        def e_sq(ph, j):
            wd = PHASES[ph][1]
            s, n = group_at(ph, j)
            if s == 0:
                dst = st[("acc", ph)]
            else:
                if j == s:
                    st[("sq", ph, s)] = sqp.tile([P, n * wd + 1], F32, name="sq", tag="sq")
                dst = st[("sq", ph, s)]
            nc.scalar.activation(out=slots(dst, ph)[:, j - s, :], in_=st[("mb", ph, j)][:], func=ACT.Square, scale=SQ_SCALE)

        waiting = []
        between = []

        def e_acc(ph, j):
            s, n = group_at(ph, j)
            if j != s + n - 1 or s == 0 or (ph == nph - 1 and s + n == NJ):
                return
            if ph == 0:
                waiting.append(s)
                return
            acc = slots(st[("acc", ph)], ph)
            nc.gpsimd.tensor_tensor(out=acc, in0=acc, in1=slots(st[("sq", ph, s)], ph), op=ALU.add)
            for h in between[0:BETWEEN]:
                h()
            rest = between[BETWEEN:]
            between.clear()
            between.extend(rest)

        def acc_after_vector():
            for s in waiting:
                acc, sq = st[("acc", 0)], st[("sq", 0, s)]
                n = group_of(0) * PHASES[0][1]
                nc.vector.memset(sq[:, n : n + 1], 0.0)
                nc.gpsimd.tensor_tensor(out=acc[:], in0=acc[:], in1=sq[:], op=ALU.add)
            waiting.clear()

        def phase_tiles(ph):
            c0, wd, nt = PHASES[ph]
            for nm in ("rmax", "rmin", "vs", "tb", "q"):
                st[(nm, ph)] = keep.tile([P, wd], F32, name="%s%d" % (nm, ph))
            st[("m0", ph)] = st[("q", ph)]
            st[("acc", ph)] = keep.tile([P, group_of(ph) * wd + 1], F32, name="acc%d" % ph)
            nc.vector.memset(st[("acc", ph)][:, group_of(ph) * wd : group_of(ph) * wd + 1], 0.0)
            if nt:
                st[("srcm", ph)] = keep.tile([P, nt], F32, name="srcm%d" % ph)
                st[("srcs", ph)] = keep.tile([P, nt], F32, name="srcs%d" % ph)
                if ph % 2 == 0:
                    st[("ts", ph)] = ps_ts.tile([P, nt], F32, name="ts", tag="ts")
                else:
                    st[("ts", ph)] = ps_tp.tile([P, nt], F32, name="tp", tag="tp")

        def x_product(w, ph, n):
            acc = ps_x.tile([P, n], F32, name="px", tag="px")
            for g in range(2):
                mx(acc[:], xc[:, g * P : (g + 1) * P], xs[:, g * P : (g + 1) * P], (w, g, ph), n, g == 0, g == 1)
            return acc

        def src_a(ph):
            nt = PHASES[ph][2]
            if nt:
                nc.scalar.copy(out=st[("srcs", ph)][:], in_=x_product(1, ph, nt)[:])

        def src_b(ph):
            nt = PHASES[ph][2]
            if nt:
                sm = ps_x.tile([P, nt], F32, name="px", tag="px")
                nc.tensor.matmul(out=sm[:], lhsT=sel[:], rhs=st[("srcs", ph)][:], start=True, stop=True)
                nc.scalar.copy(out=st[("srcm", ph)][:], in_=sm[:])

        def tgt(ph):
            c0, wd, nt = PHASES[ph]
            tb = st[("tb", ph)]
            nc.scalar.copy(out=tb[:], in_=x_product(0, ph, wd)[:])
            nc.gpsimd.tensor_tensor(out=tb[:], in0=tb[:], in1=b_bc[:, c0 : c0 + wd], op=ALU.add)

        def fin_mean_ts(fin, ph):
            c0, wd, nt = PHASES[ph]
            a = st["one"].tile([P, wd], F32, name="a%d" % ph)
            st[("a", ph)] = a
            if nt:
                nc.vector.scalar_tensor_tensor(
                    out=a[:, 0:nt], in0=st[("ts", ph)][:], scalar=1.0 / NJ, in1=st[("srcm", ph)][:], op0=ALU.mult, op1=ALU.add
                )

        def fin_mean_vs(fin, ph):
            c0, wd, nt = PHASES[ph]
            a = st[("a", ph)]
            a2 = fin.tile([P, wd], F32, name="a2", tag="a2")
            if nt:
                nc.scalar.activation(out=a2[:, 0:nt], in_=a[:, 0:nt], func=ACT.Square)
            if nt < wd:
                nc.scalar.activation(out=a2[:, nt:wd], in_=st[("vs", ph)][:, nt:wd], func=ACT.Square, scale=1.0 / NJ)
                nc.scalar.mul(out=a[:, nt:wd], in_=st[("vs", ph)][:, nt:wd], mul=1.0 / NJ)
            st[("a2", ph)] = a2

        def fin_mean(fin, ph):
            fin_mean_ts(fin, ph)
            fin_mean_vs(fin, ph)

        def fin_q(eng, ph):
            acc = slots(st[("acc", ph)], ph)
            if group_of(ph) == 4:
                eng.tensor_tensor(out=acc[:, 0:2, :], in0=acc[:, 0:2, :], in1=acc[:, 2:4, :], op=ALU.add)
            eng.tensor_tensor(out=st[("q", ph)][:], in0=acc[:, 0, :], in1=acc[:, 1, :], op=ALU.add)

        def fin_minmax(eng, O, ph):
            c0, wd, nt = PHASES[ph]
            cols = slice(c0, c0 + wd)
            tb = st[("tb", ph)]
            eng.tensor_tensor(out=O[:, 2, cols], in0=st[("rmax", ph)][:], in1=tb[:], op=ALU.add)
            eng.tensor_tensor(out=O[:, 1, cols], in0=st[("rmin", ph)][:], in1=tb[:], op=ALU.add)

        def fin_std(eng, fin, O, ph):
            c0, wd, nt = PHASES[ph]
            var = fin.tile([P, wd], F32, name="var", tag="var")
            eng.tensor_tensor(out=var[:], in0=st[("q", ph)][:], in1=st[("a2", ph)][:], op=ALU.subtract)
            st[("var", ph)] = var

        def fin_sqrt(O, ph):
            c0, wd, nt = PHASES[ph]
            var = st[("var", ph)]
            nc.scalar.activation(out=var[:], in_=var[:], func=ACT.Relu)
            nc.scalar.activation(out=O[:, 3, c0 : c0 + wd], in_=var[:], func=ACT.Sqrt, bias=eps[:, 0:1])

        def fin_meanout(eng, O, ph):
            c0, wd, nt = PHASES[ph]
            eng.tensor_tensor(out=O[:, 0, c0 : c0 + wd], in0=st[("a", ph)][:], in1=st[("tb", ph)][:], op=ALU.add)

        def fin_amax(O, ph, n, k):
            c0, wd, nt = PHASES[ph]
            nc.vector.tensor_reduce(
                out=pm[:, 3 * ph + n : 3 * ph + n + 1], in_=O[:, k, c0 : c0 + wd], axis=AX.X, op=ALU.max, apply_absolute_value=True
            )

        def fin_store(O, ph):
            c0, wd, nt = PHASES[ph]
            nc.sync.dma_start(out=o0[:, 1:4, c0 : c0 + wd], in_=O[:, 1:4, c0 : c0 + wd])

        def wd_of(ph):
            return PHASES[ph][1]

        def run_phase(ph, prep, step_hooks, bank_hooks, early_hooks):
            for s in range(NJ // 2):
                prep(s)
                for h in step_hooks.get(s, ()):
                    h()
                for jj in range(2):
                    j = 2 * s + jj
                    if not (ph == 0 and s == 0):
                        mm_e(ph, j)
                    mm_x(ph, j)
                    if ph == nph - 1 and j == NJ - 1:
                        mm_ts(ph, j, True)
                    for h in early_hooks.get(j, ()):
                        h()
                    e_vec(ph, j)
                    e_sq(ph, j)
                    e_acc(ph, j)
                    for h in bank_hooks.get(j, ()):
                        h()

        def own_hooks(ph):
            return {1: [lambda: src_a(ph)], 3: [lambda: src_b(ph)], (NJ // 2 - 1 if ph == 0 else 5): [lambda: tgt(ph)]}

        lazy = [(0, 0, 0), (0, 1, 0)]
        for ph in range(1, nph):
            lazy.extend([(2, 0, ph), (2, 1, ph), (1, 0, ph), (1, 1, ph), (0, 0, ph), (0, 1, ph)])

        lazy_at = {}
        lazy_steps = list(range(LAZY_FIRST, NJ // 2 - 1))
        double = len(lazy) - len(lazy_steps)
        k = 0
        for n, step in enumerate(lazy_steps):
            take = 2 if n >= len(lazy_steps) - double else 1
            lazy_at[step] = lazy[k : k + take]
            k += take
        assert k == len(lazy)

        with ExitStack() as c1:
            erp = c1.enter_context(tc.tile_pool(name="erp", bufs=E_BUFS))
            egp = c1.enter_context(tc.tile_pool(name="egp", bufs=3))
            wrp = c1.enter_context(tc.tile_pool(name="wrp", bufs=4))
            wgp = c1.enter_context(tc.tile_pool(name="wgp", bufs=3))

            w_load(wrp, (2, 0, 0))
            nc.sync.dma_start(out=x_sb[:], in_=x_rows)
            e_load(erp, 0)
            w_load(wrp, (2, 1, 0))
            w_load(wrp, (1, 0, 0))
            w_load(wrp, (1, 1, 0))
            e_load(erp, 1)
            e_load(erp, 2)
            for s in range(3, E_BUFS):
                e_load(erp, s)

            nc.vector.memset(xs[:].bitcast(I32), 0)
            w_interleave(wgp, (2, 0, 0), "v")
            tpx = transpose4(x_sb[:].bitcast(F32), 0)
            nc.scalar.copy(out=xg[:].bitcast(F32), in_=tpx[:].rearrange("p g u r -> p g r u"))
            e_transpose(0)
            warm_out = ps_x.tile([P, 512], F32, name="px", tag="px")
            for n in range(N_WARM):
                nc.tensor.matmul(out=warm_out[:], lhsT=zeros[:, 0:P], rhs=zeros[:], start=True, stop=True)
            e_copy(egp, 0)
            e_load(erp, E_BUFS)
            w_interleave(wgp, (2, 1, 0), "s")
            nc.vector.quantize_mx(out=xc[:].bitcast(FP8X4), scales=xs[:], in_=xg[:].rearrange("p g r t -> p (g r t)"))
            w_quant((2, 0, 0))
            for r in range(4):
                nc.vector.tensor_copy(out=xs4[:, :, r], in_=xs[:])
            e_quant(0)
            x_repeat(0)
            w_quant((2, 1, 0))
            w_interleave(wgp, (1, 0, 0), "v")
            w_interleave(wgp, (1, 1, 0), "s")
            e_transpose(1)
            e_copy(egp, 1)
            e_load(erp, E_BUFS + 1)
            w_quant((1, 0, 0))
            w_quant((1, 1, 0))
            for s in range(W_LEAD):
                for u in lazy_at.get(s, ()):
                    w_load(wrp, u)
            phase_tiles(0)
            mm_e(0, 0)
            mm_e(0, 1)

            def prep0(s):
                if s + 2 < NJ // 2:
                    e_transpose(s + 2)
                    e_copy(egp, s + 2)
                    if s + 2 + E_BUFS < NJ // 2:
                        e_load(erp, s + 2 + E_BUFS)
                for u in lazy_at.get(s + W_LEAD, ()):
                    w_load(wrp, u)
                if s == BIAS_STEP:
                    nc.sync.dma_start(out=b_bc[:], in_=b_pre.partition_broadcast(P))
                for u in lazy_at.get(s, ()):
                    w_interleave(wgp, u, "s")
                for u in lazy_at.get(s - 1, ()):
                    w_quant(u)
                if s + 1 < NJ // 2:
                    e_quant(s + 1)
                for c in range(1, len(XCH)):
                    if XSTEP[c] == s:
                        x_repeat(c)
                acc_after_vector()

            run_phase(0, prep0, own_hooks(0), {}, {})
            acc_after_vector()

        with ExitStack() as c2:
            fin = c2.enter_context(tc.tile_pool(name="fin", bufs=2))
            one = c2.enter_context(tc.tile_pool(name="one", bufs=1))
            st["one"] = one
            O = one.tile([P, 4, F], F32, name="O")
            o8 = one.tile([P, 4 * F], FP8, name="o8")

            def at_start(ph):
                fin_q(nc.gpsimd, ph)

            def after_sum(ph):
                fin_mean(fin, ph)
                fin_std(nc.gpsimd, fin, O, ph)
                c0, wd, nt = PHASES[ph]
                cols = slice(c0, c0 + wd)
                tb = st[("tb", ph)]
                between.extend([
                    lambda: nc.gpsimd.tensor_tensor(out=O[:, 2, cols], in0=st[("rmax", ph)][:], in1=tb[:], op=ALU.add),
                    lambda: nc.gpsimd.tensor_tensor(out=O[:, 1, cols], in0=st[("rmin", ph)][:], in1=tb[:], op=ALU.add),
                ])
                if BETWEEN == 0:
                    for h in between:
                        h()
                    between.clear()

            def later(ph):
                for n, k in enumerate((2, 1, 3)):
                    fin_amax(O, ph, n, k)
                fin_store(O, ph)

            def hooks_for(ph):
                steps = own_hooks(ph)
                banks = {0: [lambda: at_start(ph - 1)], LATER - 2: [lambda: fin_sqrt(O, ph - 1)], LATER: [lambda: later(ph - 1)]}
                n = len(LATE_SUM) if ph == 1 else 0
                for k in range(n):
                    banks.setdefault(k, []).append(lambda k=k: mm_ts(0, LATE_SUM[k], True))
                banks.setdefault(n, []).append(lambda: after_sum(ph - 1))
                return steps, banks

            for ph in range(1, nph):
                phase_tiles(ph)
                steps, banks = hooks_for(ph)
                run_phase(ph, lambda s: None, steps, banks, {})

            ph = nph - 1
            c0, wd, nt = PHASES[ph]
            cols = slice(c0, c0 + wd)
            tb = st[("tb", ph)]
            q = st[("q", ph)]
            sql = slots(st[("sq", ph, NJ - group_of(ph))], ph)
            var = fin.tile([P, wd], F32, name="var", tag="var")
            sd = one.tile([P, wd + 1], F32, name="sd")
            sc1 = one.tile([P, 4], F32, name="sc1")
            accl = slots(st[("acc", ph)], ph)
            nc.vector.tensor_tensor(out=O[:, 2, cols], in0=st[("rmax", ph)][:], in1=tb[:], op=ALU.add)
            nc.vector.tensor_tensor(out=O[:, 1, cols], in0=st[("rmin", ph)][:], in1=tb[:], op=ALU.add)
            nc.sync.dma_start(out=o0[:, 1:3, cols], in_=O[:, 1:3, cols])
            nc.vector.tensor_tensor(out=sql, in0=sql, in1=accl, op=ALU.add)
            fin_mean_ts(fin, ph)
            fin_mean_vs(fin, ph)
            nc.vector.tensor_tensor(out=sql[:, 0:2, :], in0=sql[:, 0:2, :], in1=sql[:, 2:4, :], op=ALU.add)
            fin_amax(O, ph, 0, 2)
            nc.vector.tensor_tensor(out=sql[:, 0, :], in0=sql[:, 0, :], in1=sql[:, 1, :], op=ALU.add)
            fin_amax(O, ph, 1, 1)
            nc.vector.tensor_tensor(out=var[:], in0=sql[:, 0, :], in1=st[("a2", ph)][:], op=ALU.subtract)
            nc.vector.tensor_reduce(out=sd[:, wd : wd + 1], in_=pm[:], axis=AX.X, op=ALU.max)
            nc.vector.tensor_scalar(out=var[:], in0=var[:], scalar1=0.0, scalar2=EPS_STD, op0=ALU.max, op1=ALU.add)
            nc.scalar.activation(out=sd[:, 0:wd], in_=var[:], func=ACT.Sqrt)
            nc.scalar.copy(out=O[:, 3, cols], in_=sd[:, 0:wd])
            for p in range(1, nph):
                fin_meanout(nc.vector, O, p)

            nc.vector.tensor_reduce(out=sc1[:, 0:1], in_=sd[:], axis=AX.X, op=ALU.max)
            nc.sync.dma_start(out=o0[:, 0, PHASES[1][0] : F], in_=O[:, 0, PHASES[1][0] : F])
            nc.sync.dma_start(out=o0[:, 3, cols], in_=O[:, 3, cols])
            am = ps_x.tile([P, P], F32, name="px", tag="px")
            nc.tensor.transpose(am[:], sc1[:, 0:1].to_broadcast([P, P]), ident[:])
            fin_meanout(nc.vector, O, 0)
            nc.sync.dma_start(out=o0[:, 0, 0 : PHASES[0][1]], in_=O[:, 0, 0 : PHASES[0][1]])
            spread = one.tile([P, P], F32, name="spread")
            nc.vector.tensor_scalar(
                out=spread[:], in0=am[:], scalar1=1.0 / 448.0, scalar2=None, op0=ALU.mult, op1=ALU.max, accum_out=sc1[:, 1:2]
            )
            nc.vector.reciprocal(out=sc1[:, 2:3], in_=sc1[:, 1:2])
            fac = sc1[:, 2:3]

            flat = O[:].rearrange("p k f -> p (k f)")
            vh = VCOLS // 2
            sh = (4 * F - VCOLS) // 2
            for h in range(2):
                va = h * vh
                sa = VCOLS + h * sh
                nc.vector.tensor_scalar(
                    out=o8[:, va : va + vh], in0=flat[:, va : va + vh], scalar1=fac, scalar2=None, op0=ALU.mult, saturate=False
                )
                nc.scalar.activation(
                    out=o8[:, sa : sa + sh], in_=flat[:, sa : sa + sh], func=ACT.Identity, scale=fac, bias=zero[:, 0:1], saturate=False
                )
                nc.sync.dma_start(out=o1[:, va : va + vh], in_=o8[:, va : va + vh].bitcast(U8))
                nc.sync.dma_start(out=o1[:, sa : sa + sh], in_=o8[:, sa : sa + sh].bitcast(U8))
